import numpy as np
import ml_dtypes


def mxq(x, axis, fmt="e4m3"):
    dtype, down = {"e4m3": (ml_dtypes.float8_e4m3fn, 7), "e5m2": (ml_dtypes.float8_e5m2, 14)}[fmt]
    v = np.moveaxis(np.asarray(x, np.float32).astype(ml_dtypes.bfloat16).astype(np.float64), axis, -1)
    blocks = v.reshape(v.shape[:-1] + (-1, 32))
    amax = np.abs(blocks).max(-1, keepdims=True)
    byte = np.maximum(np.where(amax > 0, np.frexp(amax)[1] - 1 + 127, 0) - down, 1)
    scale = np.exp2(byte - 127.0)
    codes = (blocks / scale).astype(np.float32).astype(dtype).astype(np.float64)
    return np.moveaxis((codes * scale).reshape(v.shape), -1, axis)


WIDE = False


def mx_kscale(k):
    if not WIDE:
        return np.ones(k)
    levels = np.array([10, -10, 5, -5, 0])
    a = np.random.permutation(np.resize(levels, k // 512 * 4)).reshape(k // 512, 4)
    idx = np.arange(k)
    return np.exp2(a[idx // 512, idx % 128 // 32])


BF16 = ml_dtypes.bfloat16


def bf(x):
    return np.asarray(x, np.float32).astype(BF16)


def f64(x):
    return np.asarray(x).astype(np.float64)


E2M1 = np.array([0.0, 0.5, 1.0, 1.5, 2.0, 3.0, 4.0, 6.0, -0.0, -0.5, -1.0, -1.5, -2.0, -3.0, -4.0, -6.0])


def pack_weight(w, fmt):
    k, n = w.shape
    w = f64(bf(w)).reshape(k // 32, 32, n)
    amax = np.abs(w).max(1)
    if fmt == "e4m3":
        byte = np.frexp(amax)[1] - 1 + 127 - 7
    else:
        mant, ex = np.frexp(amax / 6.0)
        byte = np.where(mant > 0.5, ex, ex - 1) + 127
    byte = np.clip(np.where(amax > 0, byte, 1), 1, 254)
    scaled = (w * np.exp2(127.0 - byte)[:, None, :]).reshape(k, n).astype(np.float32)
    by_word = np.ascontiguousarray(scaled.reshape(k // 512, 128, 4, n).transpose(0, 1, 3, 2))
    if fmt == "e4m3":
        words = by_word.astype(ml_dtypes.float8_e4m3fn).view(np.uint8)
    else:
        c = by_word.astype(ml_dtypes.float4_e2m1fn).view(np.uint8) & 0xF
        words = c[..., 0::2] | (c[..., 1::2] << 4)
    return np.ascontiguousarray(words), np.ascontiguousarray(byte.astype(np.uint8).reshape(k // 512, 16, n))


def unpack_weight(words, scales, fmt):
    g, p, n, _ = words.shape
    if fmt == "e4m3":
        vals = np.ascontiguousarray(words).view(ml_dtypes.float8_e4m3fn).astype(np.float64)
    else:
        nib = np.empty((g, p, n, 4), np.uint8)
        nib[..., 0::2] = words & 0xF
        nib[..., 1::2] = words >> 4
        vals = E2M1[nib]
    vals = vals * np.repeat(np.exp2(scales.astype(np.float64) - 127.0), 8, axis=1)[..., None]
    return vals.transpose(0, 1, 3, 2).reshape(g * 512, n)


B, S, D, H, KVH, DH, F = 2, 2048, 512, 8, 2, 128, 512
EPS = 1e-6
E = H * DH


def rms_norm(v, eps):
    return v / np.sqrt(np.mean(np.square(v), axis=-1, keepdims=True) + eps)


def setup_inputs():
    s = mx_kscale(E)
    y_attn = bf(np.random.standard_normal((B, H, S, DH)) * 0.35 * s.reshape(H, 1, DH))
    x = bf(np.random.standard_normal((B, S, D)))
    w_o = np.random.standard_normal((D, E)) / np.sqrt(E) / s[None, :]
    attn_scale = bf(1.0 + 0.1 * np.random.standard_normal(D))
    w_fc = np.random.standard_normal((F, D)) / np.sqrt(D)
    w_o_words, w_o_scales = pack_weight(np.ascontiguousarray(w_o.T), "e4m3")
    w_fc_words, w_fc_scales = pack_weight(np.ascontiguousarray(w_fc.T), "e4m3")
    return {"y_attn": y_attn,
            "x": x,
            "w_o_words": w_o_words,
            "w_o_scales": w_o_scales,
            "attn_scale": attn_scale,
            "w_fc_words": w_fc_words,
            "w_fc_scales": w_fc_scales}


def reference(y_attn, x, w_o_words, w_o_scales, attn_scale, w_fc_words, w_fc_scales):
    yc = f64(y_attn).transpose(0, 2, 1, 3).reshape(B, S, E)
    attn_out = mxq(yc, 2, "e4m3") @ unpack_weight(w_o_words, w_o_scales, "e4m3")
    x_mid = f64(x) + f64(attn_scale)[None, None, :] * attn_out
    h = mxq(rms_norm(x_mid, EPS), 2, "e4m3") @ unpack_weight(w_fc_words, w_fc_scales, "e4m3")
    h = np.square(np.maximum(h, 0.0))
    return x_mid, h

@@ -1,0 +1,222 @@
+from contextlib import ExitStack
+
+import concourse.mybir as mybir
+from concourse.masks import make_identity
+
+BF16 = mybir.dt.bfloat16
+F32 = mybir.dt.float32
+I32 = mybir.dt.int32
+U32 = mybir.dt.uint32
+U8 = mybir.dt.uint8
+FP8X4 = mybir.dt.float8_e4m3fn_x4
+ALU = mybir.AluOpType
+ACT = mybir.ActivationFunctionType
+
+B, S, D, H, DH, F = 2, 2048, 512, 8, 128, 512
+E = H * DH
+EPS = 1e-6
+FLOPS = 2 * B * S * E * D + 2 * B * S * D * F
+
+P = 128
+PACK = 4
+K_PASS = P * PACK
+KG = E // K_PASS
+SLOTS = S // P
+CHUNK = 4
+PAIR = 2
+CHUNKS = B * SLOTS // CHUNK
+PAIRS = B * SLOTS // PAIR
+PAIRS_PER_CHUNK = CHUNK // PAIR
+
+
+def tile_shepherdembryo_pb_t_kernel(
+    tc, y_attn, x, w_o_words, w_o_scales, attn_scale, w_fc_words, w_fc_scales, out_0, out_1
+):
+    nc = tc.nc
+    y_view = y_attn.rearrange("b h (p i) j -> b p h i j", i=SLOTS)
+    x_view = x.rearrange("b (p i) d -> b p i d", i=SLOTS)
+    x_mid_view = out_0.rearrange("b (p i) d -> b p i d", i=SLOTS)
+    h_view = out_1.rearrange("b (p i) d -> b p i d", i=SLOTS)
+
+    with ExitStack() as ctx:
+        const = ctx.enter_context(tc.tile_pool(name="const", bufs=1))
+        resident = ctx.enter_context(tc.tile_pool(name="resident", bufs=1))
+        work2 = ctx.enter_context(tc.tile_pool(name="work2", bufs=2))
+        work3 = ctx.enter_context(tc.tile_pool(name="work3", bufs=3))
+        outs = ctx.enter_context(tc.tile_pool(name="outs", bufs=5))
+        psum = ctx.enter_context(tc.psum_pool(name="psum", bufs=2))
+
+        ident_f32 = const.tile([P, P], F32)
+        make_identity(nc, ident_f32[:])
+        ident_bf16 = const.tile([P, P], BF16)
+        make_identity(nc, ident_bf16[:])
+        eps = const.tile([P, 1], F32)
+        nc.vector.memset(eps[:], EPS)
+        w_planes = const.tile([P, KG + 1, D], U8, align_bytes=64)
+        nc.vector.memset(w_planes[:].rearrange("p w n -> p (w n)").bitcast(I32), 0)
+        wo_words = const.tile([P, KG, D], U32, align_bytes=64)
+        wfc_words = const.tile([P, F], U32, align_bytes=64)
+        gain = const.tile([P, D], BF16)
+
+        y_raw = {}
+        x_sb = {}
+
+        def load_chunk(c):
+            b, first = divmod(c * CHUNK, SLOTS)
+            y_c = resident.tile([P, H, CHUNK, DH], BF16, name="y_raw%d" % c)
+            nc.sync.dma_start(out=y_c[:], in_=y_view[b, :, :, first : first + CHUNK, :])
+            x_c = resident.tile([P, CHUNK, D], BF16, name="x_sb%d" % c)
+            nc.sync.dma_start(out=x_c[:], in_=x_view[b, :, first : first + CHUNK, :])
+            y_raw[c] = y_c
+            x_sb[c] = x_c
+
+        load_chunk(0)
+        for g in range(KG):
+            nc.sync.dma_start(
+                out=wo_words[:, g, :].bitcast(I32),
+                in_=w_o_words[g].rearrange("p n t -> p (n t)").bitcast(I32),
+            )
+        for quad in range(4):
+            nc.sync.dma_start(
+                out=w_planes[32 * quad : 32 * quad + 4, 0:KG, :].bitcast(I32),
+                in_=w_o_scales[:, 4 * quad : 4 * quad + 4, :].rearrange("g r n -> r g n").bitcast(I32),
+            )
+        nc.sync.dma_start(out=gain[:], in_=attn_scale.partition_broadcast(P))
+        nc.sync.dma_start(
+            out=wfc_words[:].bitcast(I32),
+            in_=w_fc_words[0].rearrange("p n t -> p (n t)").bitcast(I32),
+        )
+        for quad in range(4):
+            nc.sync.dma_start(
+                out=w_planes[32 * quad : 32 * quad + 4, KG, :].bitcast(I32),
+                in_=w_fc_scales[0, 4 * quad : 4 * quad + 4, :].bitcast(I32),
+            )
+        for c in range(1, CHUNKS):
+            load_chunk(c)
+
+        y_tok = {}
+        y_mx = {}
+        xn_sb = {}
+        xn_mx = {}
+
+        def transpose_y(q):
+            c, half = divmod(q, PAIRS_PER_CHUNK)
+            if half == 0:
+                y_c = work2.tile([P, CHUNK, H, DH], BF16, name="y_tok")
+                nc.vector.tensor_copy(out=y_c[:], in_=y_raw[c][:].rearrange("p h i j -> p i h j"))
+                y_tok[c] = y_c
+            y_grouped = work2.tile([P, PAIR, KG, P, PACK], BF16, align_bytes=64)
+            for a in range(PAIR):
+                words = y_tok[c][:, half * PAIR + a].rearrange("p h j -> p (h j)").bitcast(F32)
+                y_t = psum.tile([P, KG, 2, P], F32)
+                for g in range(KG):
+                    for u in range(2):
+                        nc.tensor.transpose(
+                            y_t[:, g, u, :],
+                            words[:, (K_PASS // 2) * g + u : (K_PASS // 2) * (g + 1) : 2],
+                            ident_f32[:],
+                        )
+                nc.vector.tensor_copy(
+                    out=y_grouped[:, a]
+                    .rearrange("p g r t -> p (g r t)")
+                    .bitcast(F32)
+                    .rearrange("p (g r u) -> p g r u", g=KG, u=2),
+                    in_=y_t[:].rearrange("p g u r -> p g r u"),
+                )
+            y_codes = work3.tile([P, PAIR, KG, P], U32, align_bytes=64)
+            y_scales = work3.tile([P, PAIR, KG, P], U8, align_bytes=64)
+            nc.vector.quantize_mx(
+                out=y_codes[:].rearrange("p a g r -> p (a g r)").bitcast(FP8X4),
+                scales=y_scales[:].rearrange("p a g r -> p (a g r)"),
+                in_=y_grouped[:].rearrange("p a g r t -> p (a g r t)"),
+            )
+            y_mx[q] = (y_codes, y_scales)
+
+        def project_and_normalise(q):
+            c, half = divmod(q, PAIRS_PER_CHUNK)
+            b, first = divmod(q * PAIR, SLOTS)
+            y_codes, y_scales = y_mx[q]
+            scaled = work2.tile([P, PAIR, D], F32)
+            for a in range(PAIR):
+                attn = psum.tile([P, D], F32)
+                for g in range(KG):
+                    nc.tensor.matmul_mx(
+                        out=attn[:],
+                        lhsT=y_codes[:, a, g, :].bitcast(FP8X4),
+                        lhsT_scale=y_scales[:, a, g, :],
+                        rhs=wo_words[:, g, :].bitcast(FP8X4),
+                        rhs_scale=w_planes[:, g, :],
+                        start=(g == 0),
+                        stop=(g == KG - 1),
+                    )
+                nc.vector.tensor_tensor(out=scaled[:, a, :], in0=attn[:], in1=gain[:], op=ALU.mult)
+            x_mid = outs.tile([P, PAIR, D], F32)
+            nc.gpsimd.tensor_tensor(
+                out=x_mid[:],
+                in0=scaled[:],
+                in1=x_sb[c][:, half * PAIR : (half + 1) * PAIR, :],
+                op=ALU.add,
+            )
+            nc.sync.dma_start(out=x_mid_view[b, :, first : first + PAIR, :], in_=x_mid[:])
+            sumsq = work3.tile([P, PAIR], F32)
+            for a in range(PAIR):
+                squares = work2.tile([P, D], BF16)
+                nc.scalar.activation(
+                    out=squares[:], in_=x_mid[:, a, :], func=ACT.Square, accum_out=sumsq[:, a : a + 1]
+                )
+            rms = work3.tile([P, PAIR], F32)
+            nc.scalar.activation(out=rms[:], in_=sumsq[:], func=ACT.Sqrt, bias=eps[:], scale=1.0 / D)
+            rstd = work3.tile([P, PAIR], F32)
+            nc.vector.reciprocal(out=rstd[:], in_=rms[:])
+            xn = work3.tile([P, PAIR, D], BF16)
+            for a in range(PAIR):
+                nc.vector.tensor_scalar(
+                    out=xn[:, a, :], in0=x_mid[:, a, :], scalar1=rstd[:, a : a + 1], scalar2=None, op0=ALU.mult
+                )
+            xn_sb[q] = xn
+
+        def transpose_xn(q):
+            xn = xn_sb[q]
+            xn_t = psum.tile([P, PAIR, PACK, P], BF16)
+            for a in range(PAIR):
+                for t in range(PACK):
+                    nc.tensor.transpose(xn_t[:, a, t, :], xn[:, a, t:D:PACK], ident_bf16[:])
+            xn_grouped = work2.tile([P, PAIR, P, PACK], BF16, align_bytes=64)
+            nc.scalar.copy(out=xn_grouped[:], in_=xn_t[:].rearrange("p a t r -> p a r t"))
+            xn_codes = work3.tile([P, PAIR, P], U32, align_bytes=64)
+            xn_scales = work3.tile([P, PAIR, P], U8, align_bytes=64)
+            nc.vector.quantize_mx(
+                out=xn_codes[:].rearrange("p a r -> p (a r)").bitcast(FP8X4),
+                scales=xn_scales[:].rearrange("p a r -> p (a r)"),
+                in_=xn_grouped[:].rearrange("p a r t -> p (a r t)"),
+            )
+            xn_mx[q] = (xn_codes, xn_scales)
+
+        def up_project(q):
+            b, first = divmod(q * PAIR, SLOTS)
+            xn_codes, xn_scales = xn_mx[q]
+            h_sb = outs.tile([P, PAIR, F], F32)
+            for a in range(PAIR):
+                h_ps = psum.tile([P, F], F32)
+                nc.tensor.matmul_mx(
+                    out=h_ps[:],
+                    lhsT=xn_codes[:, a, :].bitcast(FP8X4),
+                    lhsT_scale=xn_scales[:, a, :],
+                    rhs=wfc_words[:].bitcast(FP8X4),
+                    rhs_scale=w_planes[:, KG, :],
+                    start=True,
+                    stop=True,
+                )
+                nc.scalar.activation(out=h_sb[:, a, :], in_=h_ps[:], func=ACT.Relu)
+            nc.scalar.activation(out=h_sb[:], in_=h_sb[:], func=ACT.Square)
+            nc.sync.dma_start(out=h_view[b, :, first : first + PAIR, :], in_=h_sb[:])
+
+        for step in range(PAIRS + 3):
+            if step < PAIRS:
+                transpose_y(step)
+            if 0 <= step - 2 < PAIRS:
+                transpose_xn(step - 2)
+            if 0 <= step - 1 < PAIRS:
+                project_and_normalise(step - 1)
+            if 0 <= step - 3 < PAIRS:
+                up_project(step - 3)

@@ -21,12 +21,17 @@ P = 128
 PACK = 4
 K_PASS = P * PACK
 KG = E // K_PASS
+HG = H // KG
 SLOTS = S // P
+TILES = B * SLOTS
 CHUNK = 4
 PAIR = 2
-CHUNKS = B * SLOTS // CHUNK
-PAIRS = B * SLOTS // PAIR
-PAIRS_PER_CHUNK = CHUNK // PAIR
+CHUNKS = TILES // CHUNK
+
+LAG_PROJECT = 2
+LAG_NORM = 3
+LAG_XN = 4
+LAG_UP = 6
 
 
 def tile_shepherdembryo_pb_t_kernel(
@@ -43,8 +48,10 @@ def tile_shepherdembryo_pb_t_kernel(
         resident = ctx.enter_context(tc.tile_pool(name="resident", bufs=1))
         work2 = ctx.enter_context(tc.tile_pool(name="work2", bufs=2))
         work3 = ctx.enter_context(tc.tile_pool(name="work3", bufs=3))
+        work4 = ctx.enter_context(tc.tile_pool(name="work4", bufs=4))
         outs = ctx.enter_context(tc.tile_pool(name="outs", bufs=5))
         psum = ctx.enter_context(tc.psum_pool(name="psum", bufs=2))
+        ctx.enter_context(tc.manual_schedule())
 
         ident_f32 = const.tile([P, P], F32)
         make_identity(nc, ident_f32[:])
@@ -94,129 +101,189 @@ def tile_shepherdembryo_pb_t_kernel(
         for c in range(1, CHUNKS):
             load_chunk(c)
 
-        y_tok = {}
+        y_sorted = {}
+        y_grouped = {}
         y_mx = {}
+        x_mid = {}
+        sumsq = {}
+        rstd = {}
         xn_sb = {}
+        xn_grouped = {}
         xn_mx = {}
+        h_psum = {}
+        h_sb = {}
 
-        def transpose_y(q):
-            c, half = divmod(q, PAIRS_PER_CHUNK)
-            if half == 0:
-                y_c = work2.tile([P, CHUNK, H, DH], BF16, name="y_tok")
-                nc.vector.tensor_copy(out=y_c[:], in_=y_raw[c][:].rearrange("p h i j -> p i h j"))
-                y_tok[c] = y_c
-            y_grouped = work2.tile([P, PAIR, KG, P, PACK], BF16, align_bytes=64)
-            for a in range(PAIR):
-                words = y_tok[c][:, half * PAIR + a].rearrange("p h j -> p (h j)").bitcast(F32)
-                y_t = psum.tile([P, KG, 2, P], F32)
-                for g in range(KG):
-                    for u in range(2):
-                        nc.tensor.transpose(
-                            y_t[:, g, u, :],
-                            words[:, (K_PASS // 2) * g + u : (K_PASS // 2) * (g + 1) : 2],
-                            ident_f32[:],
-                        )
-                nc.vector.tensor_copy(
-                    out=y_grouped[:, a]
-                    .rearrange("p g r t -> p (g r t)")
-                    .bitcast(F32)
-                    .rearrange("p (g r u) -> p g r u", g=KG, u=2),
-                    in_=y_t[:].rearrange("p g u r -> p g r u"),
-                )
-            y_codes = work3.tile([P, PAIR, KG, P], U32, align_bytes=64)
-            y_scales = work3.tile([P, PAIR, KG, P], U8, align_bytes=64)
-            nc.vector.quantize_mx(
-                out=y_codes[:].rearrange("p a g r -> p (a g r)").bitcast(FP8X4),
-                scales=y_scales[:].rearrange("p a g r -> p (a g r)"),
-                in_=y_grouped[:].rearrange("p a g r t -> p (a g r t)"),
+        def live(n):
+            return 0 <= n < TILES
+
+        def sort_y_words(c):
+            if c >= CHUNKS:
+                return
+            y_c = work2.tile([P, CHUNK, 2, H, DH // PACK], F32, name="y_sorted")
+            nc.vector.tensor_copy(
+                out=y_c[:],
+                in_=y_raw[c][:]
+                .rearrange("p h i j -> p (h i j)")
+                .bitcast(F32)
+                .rearrange("p (h i jp u) -> p i u h jp", h=H, i=CHUNK, u=2),
             )
-            y_mx[q] = (y_codes, y_scales)
+            y_sorted[c] = y_c
 
-        def project_and_normalise(q):
-            c, half = divmod(q, PAIRS_PER_CHUNK)
-            b, first = divmod(q * PAIR, SLOTS)
-            y_codes, y_scales = y_mx[q]
-            scaled = work2.tile([P, PAIR, D], F32)
-            for a in range(PAIR):
-                attn = psum.tile([P, D], F32)
-                for g in range(KG):
-                    nc.tensor.matmul_mx(
-                        out=attn[:],
-                        lhsT=y_codes[:, a, g, :].bitcast(FP8X4),
-                        lhsT_scale=y_scales[:, a, g, :],
-                        rhs=wo_words[:, g, :].bitcast(FP8X4),
-                        rhs_scale=w_planes[:, g, :],
-                        start=(g == 0),
-                        stop=(g == KG - 1),
+        def transpose_y(n):
+            if not live(n):
+                return
+            c, i = divmod(n, CHUNK)
+            y_t = psum.tile([P, KG, 2, P], F32)
+            for g in range(KG):
+                for u in range(2):
+                    nc.tensor.transpose(
+                        y_t[:, g, u, :],
+                        y_sorted[c][:, i, u, HG * g : HG * (g + 1), :].rearrange("p h jp -> p (h jp)"),
+                        ident_f32[:],
                     )
-                nc.vector.tensor_tensor(out=scaled[:, a, :], in0=attn[:], in1=gain[:], op=ALU.mult)
-            x_mid = outs.tile([P, PAIR, D], F32)
-            nc.gpsimd.tensor_tensor(
-                out=x_mid[:],
-                in0=scaled[:],
-                in1=x_sb[c][:, half * PAIR : (half + 1) * PAIR, :],
-                op=ALU.add,
+            y_g = work2.tile([P, KG, P, PACK], BF16, align_bytes=64, name="y_grouped")
+            nc.vector.tensor_copy(
+                out=y_g[:]
+                .rearrange("p g r t -> p (g r t)")
+                .bitcast(F32)
+                .rearrange("p (g r u) -> p g r u", g=KG, u=2),
+                in_=y_t[:].rearrange("p g u r -> p g r u"),
             )
-            nc.sync.dma_start(out=x_mid_view[b, :, first : first + PAIR, :], in_=x_mid[:])
-            sumsq = work3.tile([P, PAIR], F32)
-            for a in range(PAIR):
-                squares = work2.tile([P, D], BF16)
-                nc.scalar.activation(
-                    out=squares[:], in_=x_mid[:, a, :], func=ACT.Square, accum_out=sumsq[:, a : a + 1]
-                )
-            rms = work3.tile([P, PAIR], F32)
-            nc.scalar.activation(out=rms[:], in_=sumsq[:], func=ACT.Sqrt, bias=eps[:], scale=1.0 / D)
-            rstd = work3.tile([P, PAIR], F32)
-            nc.vector.reciprocal(out=rstd[:], in_=rms[:])
-            xn = work3.tile([P, PAIR, D], BF16)
-            for a in range(PAIR):
-                nc.vector.tensor_scalar(
-                    out=xn[:, a, :], in0=x_mid[:, a, :], scalar1=rstd[:, a : a + 1], scalar2=None, op0=ALU.mult
-                )
-            xn_sb[q] = xn
+            y_grouped[n] = y_g
 
-        def transpose_xn(q):
-            xn = xn_sb[q]
-            xn_t = psum.tile([P, PAIR, PACK, P], BF16)
-            for a in range(PAIR):
-                for t in range(PACK):
-                    nc.tensor.transpose(xn_t[:, a, t, :], xn[:, a, t:D:PACK], ident_bf16[:])
-            xn_grouped = work2.tile([P, PAIR, P, PACK], BF16, align_bytes=64)
-            nc.scalar.copy(out=xn_grouped[:], in_=xn_t[:].rearrange("p a t r -> p a r t"))
-            xn_codes = work3.tile([P, PAIR, P], U32, align_bytes=64)
-            xn_scales = work3.tile([P, PAIR, P], U8, align_bytes=64)
+        def quantise_y(n):
+            if not live(n):
+                return
+            y_codes = work4.tile([P, KG, P], U32, align_bytes=64)
+            y_scales = work4.tile([P, KG, P], U8, align_bytes=64)
             nc.vector.quantize_mx(
-                out=xn_codes[:].rearrange("p a r -> p (a r)").bitcast(FP8X4),
-                scales=xn_scales[:].rearrange("p a r -> p (a r)"),
-                in_=xn_grouped[:].rearrange("p a r t -> p (a r t)"),
+                out=y_codes[:].rearrange("p g r -> p (g r)").bitcast(FP8X4),
+                scales=y_scales[:].rearrange("p g r -> p (g r)"),
+                in_=y_grouped[n][:].rearrange("p g r t -> p (g r t)"),
             )
-            xn_mx[q] = (xn_codes, xn_scales)
+            y_mx[n] = (y_codes, y_scales)
 
-        def up_project(q):
-            b, first = divmod(q * PAIR, SLOTS)
-            xn_codes, xn_scales = xn_mx[q]
-            h_sb = outs.tile([P, PAIR, F], F32)
-            for a in range(PAIR):
-                h_ps = psum.tile([P, F], F32)
+        def project(n):
+            if not live(n):
+                return
+            c, i = divmod(n, CHUNK)
+            y_codes, y_scales = y_mx[n]
+            attn = psum.tile([P, D], F32)
+            for g in range(KG):
                 nc.tensor.matmul_mx(
-                    out=h_ps[:],
-                    lhsT=xn_codes[:, a, :].bitcast(FP8X4),
-                    lhsT_scale=xn_scales[:, a, :],
-                    rhs=wfc_words[:].bitcast(FP8X4),
-                    rhs_scale=w_planes[:, KG, :],
-                    start=True,
-                    stop=True,
+                    out=attn[:],
+                    lhsT=y_codes[:, g, :].bitcast(FP8X4),
+                    lhsT_scale=y_scales[:, g, :],
+                    rhs=wo_words[:, g, :].bitcast(FP8X4),
+                    rhs_scale=w_planes[:, g, :],
+                    start=(g == 0),
+                    stop=(g == KG - 1),
                 )
-                nc.scalar.activation(out=h_sb[:, a, :], in_=h_ps[:], func=ACT.Relu)
-            nc.scalar.activation(out=h_sb[:], in_=h_sb[:], func=ACT.Square)
-            nc.sync.dma_start(out=h_view[b, :, first : first + PAIR, :], in_=h_sb[:])
+            scaled = work3.tile([P, D], F32)
+            nc.vector.tensor_tensor(out=scaled[:], in0=attn[:], in1=gain[:], op=ALU.mult)
+            pair, a = divmod(n, PAIR)
+            if a == 0:
+                x_mid_pair = outs.tile([P, PAIR, D], F32)
+                x_mid[pair] = x_mid_pair
+            nc.gpsimd.tensor_tensor(out=x_mid[pair][:, a, :], in0=scaled[:], in1=x_sb[c][:, i, :], op=ALU.add)
+            if a == PAIR - 1:
+                b, first = divmod(pair * PAIR, SLOTS)
+                nc.sync.dma_start(out=x_mid_view[b, :, first : first + PAIR, :], in_=x_mid[pair][:])
 
-        for step in range(PAIRS + 3):
-            if step < PAIRS:
-                transpose_y(step)
-            if 0 <= step - 2 < PAIRS:
-                transpose_xn(step - 2)
-            if 0 <= step - 1 < PAIRS:
-                project_and_normalise(step - 1)
-            if 0 <= step - 3 < PAIRS:
-                up_project(step - 3)
+        def sum_squares(n):
+            if not live(n):
+                return
+            pair, a = divmod(n, PAIR)
+            squares = work2.tile([P, D], BF16)
+            total = work4.tile([P, 1], F32)
+            nc.scalar.activation(out=squares[:], in_=x_mid[pair][:, a, :], func=ACT.Square, accum_out=total[:])
+            sumsq[n] = total
+
+        def inverse_rms(n):
+            if not live(n):
+                return
+            inv = work4.tile([P, 1], F32)
+            nc.scalar.activation(
+                out=inv[:], in_=sumsq[n][:], func=ACT.Abs_reciprocal_sqrt, bias=eps[:], scale=1.0 / D
+            )
+            rstd[n] = inv
+
+        def normalise(n):
+            if not live(n):
+                return
+            pair, a = divmod(n, PAIR)
+            xn = work3.tile([P, D], BF16)
+            nc.scalar.activation(out=xn[:], in_=x_mid[pair][:, a, :], func=ACT.Copy, scale=rstd[n][:])
+            xn_sb[n] = xn
+
+        def transpose_xn(n):
+            if not live(n):
+                return
+            xn_t = psum.tile([P, PACK, P], BF16)
+            for t in range(PACK):
+                nc.tensor.transpose(xn_t[:, t, :], xn_sb[n][:, t:D:PACK], ident_bf16[:])
+            xn_g = work2.tile([P, P, PACK], BF16, align_bytes=64, name="xn_grouped")
+            nc.vector.tensor_copy(out=xn_g[:], in_=xn_t[:].rearrange("p t r -> p r t"))
+            xn_grouped[n] = xn_g
+
+        def quantise_xn(n):
+            if not live(n):
+                return
+            xn_codes = work4.tile([P, P], U32, align_bytes=64)
+            xn_scales = work4.tile([P, P], U8, align_bytes=64)
+            nc.vector.quantize_mx(
+                out=xn_codes[:].bitcast(FP8X4),
+                scales=xn_scales[:],
+                in_=xn_grouped[n][:].rearrange("p r t -> p (r t)"),
+            )
+            xn_mx[n] = (xn_codes, xn_scales)
+
+        def up_project(n):
+            if not live(n):
+                return
+            xn_codes, xn_scales = xn_mx[n]
+            h_ps = psum.tile([P, F], F32)
+            nc.tensor.matmul_mx(
+                out=h_ps[:],
+                lhsT=xn_codes[:].bitcast(FP8X4),
+                lhsT_scale=xn_scales[:],
+                rhs=wfc_words[:].bitcast(FP8X4),
+                rhs_scale=w_planes[:, KG, :],
+                start=True,
+                stop=True,
+            )
+            h_psum[n] = h_ps
+
+        def relu(n):
+            if not live(n):
+                return
+            pair, a = divmod(n, PAIR)
+            if a == 0:
+                h_pair = outs.tile([P, PAIR, F], F32)
+                h_sb[pair] = h_pair
+            nc.scalar.activation(out=h_sb[pair][:, a, :], in_=h_psum[n][:], func=ACT.Relu)
+
+        def square_and_store(n):
+            if not live(n):
+                return
+            pair, a = divmod(n, PAIR)
+            nc.scalar.activation(out=h_sb[pair][:, a, :], in_=h_sb[pair][:, a, :], func=ACT.Square)
+            if a == PAIR - 1:
+                b, first = divmod(pair * PAIR, SLOTS)
+                nc.sync.dma_start(out=h_view[b, :, first : first + PAIR, :], in_=h_sb[pair][:])
+
+        sort_y_words(0)
+        for n in range(TILES + LAG_UP):
+            project(n - LAG_PROJECT)
+            up_project(n - LAG_UP)
+            transpose_y(n)
+            transpose_xn(n - LAG_XN)
+            quantise_y(n)
+            quantise_xn(n - LAG_XN)
+            if n % CHUNK == 0:
+                sort_y_words(n // CHUNK + 1)
+            sum_squares(n - LAG_NORM)
+            relu(n - LAG_UP)
+            inverse_rms(n - LAG_NORM)
+            square_and_store(n - LAG_UP)
+            normalise(n - LAG_NORM)

@@ -21,7 +21,6 @@ P = 128
 PACK = 4
 K_PASS = P * PACK
 KG = E // K_PASS
-HG = H // KG
 SLOTS = S // P
 TILES = B * SLOTS
 CHUNK = 4
@@ -49,7 +48,7 @@ def tile_shepherdembryo_pb_t_kernel(
         work2 = ctx.enter_context(tc.tile_pool(name="work2", bufs=2))
         work3 = ctx.enter_context(tc.tile_pool(name="work3", bufs=3))
         work4 = ctx.enter_context(tc.tile_pool(name="work4", bufs=4))
-        outs = ctx.enter_context(tc.tile_pool(name="outs", bufs=5))
+        outs = ctx.enter_context(tc.tile_pool(name="outs", bufs=7))
         psum = ctx.enter_context(tc.psum_pool(name="psum", bufs=2))
         ctx.enter_context(tc.manual_schedule())
 
@@ -65,19 +64,23 @@ def tile_shepherdembryo_pb_t_kernel(
         wfc_words = const.tile([P, F], U32, align_bytes=64)
         gain = const.tile([P, D], BF16)
 
-        y_raw = {}
+        y_sb = {}
         x_sb = {}
 
-        def load_chunk(c):
+        def load_y(n):
+            b, i = divmod(n, SLOTS)
+            y_n = resident.tile([P, H, DH], BF16, name="y_sb%d" % n)
+            nc.sync.dma_start(out=y_n[:], in_=y_view[b, :, :, i, :])
+            y_sb[n] = y_n
+
+        def load_x(c):
             b, first = divmod(c * CHUNK, SLOTS)
-            y_c = resident.tile([P, H, CHUNK, DH], BF16, name="y_raw%d" % c)
-            nc.sync.dma_start(out=y_c[:], in_=y_view[b, :, :, first : first + CHUNK, :])
             x_c = resident.tile([P, CHUNK, D], BF16, name="x_sb%d" % c)
             nc.sync.dma_start(out=x_c[:], in_=x_view[b, :, first : first + CHUNK, :])
-            y_raw[c] = y_c
             x_sb[c] = x_c
 
-        load_chunk(0)
+        load_y(0)
+        load_y(1)
         for g in range(KG):
             nc.sync.dma_start(
                 out=wo_words[:, g, :].bitcast(I32),
@@ -89,6 +92,9 @@ def tile_shepherdembryo_pb_t_kernel(
                 in_=w_o_scales[:, 4 * quad : 4 * quad + 4, :].rearrange("g r n -> r g n").bitcast(I32),
             )
         nc.sync.dma_start(out=gain[:], in_=attn_scale.partition_broadcast(P))
+        load_x(0)
+        load_y(2)
+        load_y(3)
         nc.sync.dma_start(
             out=wfc_words[:].bitcast(I32),
             in_=w_fc_words[0].rearrange("p n t -> p (n t)").bitcast(I32),
@@ -99,9 +105,10 @@ def tile_shepherdembryo_pb_t_kernel(
                 in_=w_fc_scales[0, 4 * quad : 4 * quad + 4, :].bitcast(I32),
             )
         for c in range(1, CHUNKS):
-            load_chunk(c)
+            load_x(c)
+            for n in range(c * CHUNK, (c + 1) * CHUNK):
+                load_y(n)
 
-        y_sorted = {}
         y_grouped = {}
         y_mx = {}
         x_mid = {}
@@ -116,29 +123,16 @@ def tile_shepherdembryo_pb_t_kernel(
         def live(n):
             return 0 <= n < TILES
 
-        def sort_y_words(c):
-            if c >= CHUNKS:
-                return
-            y_c = work2.tile([P, CHUNK, 2, H, DH // PACK], F32, name="y_sorted")
-            nc.vector.tensor_copy(
-                out=y_c[:],
-                in_=y_raw[c][:]
-                .rearrange("p h i j -> p (h i j)")
-                .bitcast(F32)
-                .rearrange("p (h i jp u) -> p i u h jp", h=H, i=CHUNK, u=2),
-            )
-            y_sorted[c] = y_c
-
         def transpose_y(n):
             if not live(n):
                 return
-            c, i = divmod(n, CHUNK)
+            words = y_sb[n][:].rearrange("p h j -> p (h j)").bitcast(F32)
             y_t = psum.tile([P, KG, 2, P], F32)
             for g in range(KG):
                 for u in range(2):
                     nc.tensor.transpose(
                         y_t[:, g, u, :],
-                        y_sorted[c][:, i, u, HG * g : HG * (g + 1), :].rearrange("p h jp -> p (h jp)"),
+                        words[:, (K_PASS // 2) * g + u : (K_PASS // 2) * (g + 1) : 2],
                         ident_f32[:],
                     )
             y_g = work2.tile([P, KG, P, PACK], BF16, align_bytes=64, name="y_grouped")
@@ -272,7 +266,6 @@ def tile_shepherdembryo_pb_t_kernel(
                 b, first = divmod(pair * PAIR, SLOTS)
                 nc.sync.dma_start(out=h_view[b, :, first : first + PAIR, :], in_=h_sb[pair][:])
 
-        sort_y_words(0)
         for n in range(TILES + LAG_UP):
             project(n - LAG_PROJECT)
             up_project(n - LAG_UP)
@@ -280,8 +273,6 @@ def tile_shepherdembryo_pb_t_kernel(
             transpose_xn(n - LAG_XN)
             quantise_y(n)
             quantise_xn(n - LAG_XN)
-            if n % CHUNK == 0:
-                sort_y_words(n // CHUNK + 1)
             sum_squares(n - LAG_NORM)
             relu(n - LAG_UP)
             inverse_rms(n - LAG_NORM)

@@ -31,6 +31,7 @@ LAG_PROJECT = 2
 LAG_NORM = 3
 LAG_XN = 4
 LAG_UP = 6
+LOAD_AHEAD = 6
 
 
 def tile_shepherdembryo_pb_t_kernel(
@@ -54,8 +55,6 @@ def tile_shepherdembryo_pb_t_kernel(
 
         ident_f32 = const.tile([P, P], F32)
         make_identity(nc, ident_f32[:])
-        ident_bf16 = const.tile([P, P], BF16)
-        make_identity(nc, ident_bf16[:])
         eps = const.tile([P, 1], F32)
         nc.vector.memset(eps[:], EPS)
         w_planes = const.tile([P, KG + 1, D], U8, align_bytes=64)
@@ -68,12 +67,16 @@ def tile_shepherdembryo_pb_t_kernel(
         x_sb = {}
 
         def load_y(n):
+            if n >= TILES:
+                return
             b, i = divmod(n, SLOTS)
             y_n = resident.tile([P, H, DH], BF16, name="y_sb%d" % n)
             nc.sync.dma_start(out=y_n[:], in_=y_view[b, :, :, i, :])
             y_sb[n] = y_n
 
         def load_x(c):
+            if c >= CHUNKS:
+                return
             b, first = divmod(c * CHUNK, SLOTS)
             x_c = resident.tile([P, CHUNK, D], BF16, name="x_sb%d" % c)
             nc.sync.dma_start(out=x_c[:], in_=x_view[b, :, first : first + CHUNK, :])
@@ -93,8 +96,8 @@ def tile_shepherdembryo_pb_t_kernel(
             )
         nc.sync.dma_start(out=gain[:], in_=attn_scale.partition_broadcast(P))
         load_x(0)
-        load_y(2)
-        load_y(3)
+        for n in range(2, LOAD_AHEAD):
+            load_y(n)
         nc.sync.dma_start(
             out=wfc_words[:].bitcast(I32),
             in_=w_fc_words[0].rearrange("p n t -> p (n t)").bitcast(I32),
@@ -104,17 +107,15 @@ def tile_shepherdembryo_pb_t_kernel(
                 out=w_planes[32 * quad : 32 * quad + 4, KG, :].bitcast(I32),
                 in_=w_fc_scales[0, 4 * quad : 4 * quad + 4, :].bitcast(I32),
             )
-        for c in range(1, CHUNKS):
-            load_x(c)
-            for n in range(c * CHUNK, (c + 1) * CHUNK):
-                load_y(n)
 
         y_grouped = {}
         y_mx = {}
         x_mid = {}
         sumsq = {}
         rstd = {}
-        xn_sb = {}
+        x_mid_t = {}
+        rstd_psum = {}
+        rstd_row = {}
         xn_grouped = {}
         xn_mx = {}
         h_psum = {}
@@ -202,22 +203,41 @@ def tile_shepherdembryo_pb_t_kernel(
             )
             rstd[n] = inv
 
-        def normalise(n):
+        def transpose_x_mid(n):
             if not live(n):
                 return
             pair, a = divmod(n, PAIR)
-            xn = work3.tile([P, D], BF16)
-            nc.scalar.activation(out=xn[:], in_=x_mid[pair][:, a, :], func=ACT.Copy, scale=rstd[n][:])
-            xn_sb[n] = xn
+            xm_t = psum.tile([P, PACK, P], F32)
+            for t in range(PACK):
+                nc.tensor.transpose(xm_t[:, t, :], x_mid[pair][:, a, t:D:PACK], ident_f32[:])
+            x_mid_t[n] = xm_t
 
-        def transpose_xn(n):
+        def spread_inverse_rms(n):
             if not live(n):
                 return
-            xn_t = psum.tile([P, PACK, P], BF16)
-            for t in range(PACK):
-                nc.tensor.transpose(xn_t[:, t, :], xn_sb[n][:, t:D:PACK], ident_bf16[:])
+            row_ps = psum.tile([P, P], F32, bufs=1)
+            nc.tensor.matmul(
+                out=row_ps[:], lhsT=rstd[n][:].to_broadcast([P, P]), rhs=ident_f32[:], start=True, stop=True
+            )
+            rstd_psum[n] = row_ps
+
+        def copy_inverse_rms(n):
+            if not live(n):
+                return
+            row = work3.tile([P, P], F32)
+            nc.scalar.copy(out=row[:], in_=rstd_psum[n][:])
+            rstd_row[n] = row
+
+        def normalise(n):
+            if not live(n):
+                return
             xn_g = work2.tile([P, P, PACK], BF16, align_bytes=64, name="xn_grouped")
-            nc.vector.tensor_copy(out=xn_g[:], in_=xn_t[:].rearrange("p t r -> p r t"))
+            nc.vector.tensor_tensor(
+                out=xn_g[:],
+                in0=x_mid_t[n][:].rearrange("p t r -> p r t"),
+                in1=rstd_row[n][:].unsqueeze(2).to_broadcast([P, P, PACK]),
+                op=ALU.mult,
+            )
             xn_grouped[n] = xn_g
 
         def quantise_xn(n):
@@ -236,7 +256,7 @@ def tile_shepherdembryo_pb_t_kernel(
             if not live(n):
                 return
             xn_codes, xn_scales = xn_mx[n]
-            h_ps = psum.tile([P, F], F32)
+            h_ps = psum.tile([P, F], F32, bufs=1)
             nc.tensor.matmul_mx(
                 out=h_ps[:],
                 lhsT=xn_codes[:].bitcast(FP8X4),
@@ -267,14 +287,19 @@ def tile_shepherdembryo_pb_t_kernel(
                 nc.sync.dma_start(out=h_view[b, :, first : first + PAIR, :], in_=h_sb[pair][:])
 
         for n in range(TILES + LAG_UP):
+            load_y(n + LOAD_AHEAD)
+            if n % CHUNK == 0:
+                load_x(n // CHUNK + 1)
             project(n - LAG_PROJECT)
             up_project(n - LAG_UP)
+            spread_inverse_rms(n - LAG_XN)
             transpose_y(n)
-            transpose_xn(n - LAG_XN)
+            transpose_x_mid(n - LAG_NORM)
+            sum_squares(n - LAG_NORM)
+            copy_inverse_rms(n - LAG_XN)
+            normalise(n - LAG_XN)
             quantise_y(n)
             quantise_xn(n - LAG_XN)
-            sum_squares(n - LAG_NORM)
             relu(n - LAG_UP)
             inverse_rms(n - LAG_NORM)
             square_and_store(n - LAG_UP)
-            normalise(n - LAG_NORM)

@@ -29,8 +29,10 @@ CHUNKS = TILES // CHUNK
 
 LAG_PROJECT = 2
 LAG_NORM = 3
-LAG_XN = 4
-LAG_UP = 6
+LAG_SCALE = 4
+LAG_XN = 5
+LAG_QUANTISE_XN = 6
+LAG_UP = 7
 LOAD_AHEAD = 6
 
 
@@ -113,9 +115,8 @@ def tile_shepherdembryo_pb_t_kernel(
         x_mid = {}
         sumsq = {}
         rstd = {}
-        x_mid_t = {}
-        rstd_psum = {}
-        rstd_row = {}
+        xn = {}
+        xn_t = {}
         xn_grouped = {}
         xn_mx = {}
         h_psum = {}
@@ -203,40 +204,36 @@ def tile_shepherdembryo_pb_t_kernel(
             )
             rstd[n] = inv
 
-        def transpose_x_mid(n):
+        def scale_xn(n):
             if not live(n):
                 return
             pair, a = divmod(n, PAIR)
-            xm_t = psum.tile([P, PACK, P], F32)
-            for t in range(PACK):
-                nc.tensor.transpose(xm_t[:, t, :], x_mid[pair][:, a, t:D:PACK], ident_f32[:])
-            x_mid_t[n] = xm_t
-
-        def spread_inverse_rms(n):
-            if not live(n):
-                return
-            row_ps = psum.tile([P, P], F32, bufs=1)
-            nc.tensor.matmul(
-                out=row_ps[:], lhsT=rstd[n][:].to_broadcast([P, P]), rhs=ident_f32[:], start=True, stop=True
+            xn_n = work3.tile([P, 2, P, 2], BF16, align_bytes=64, name="xn")
+            nc.vector.tensor_scalar(
+                out=xn_n[:],
+                in0=x_mid[pair][:, a, :].rearrange("r (p u e) -> r u p e", u=2, e=2),
+                scalar1=rstd[n][:],
+                scalar2=None,
+                op0=ALU.mult,
             )
-            rstd_psum[n] = row_ps
+            xn[n] = xn_n
 
-        def copy_inverse_rms(n):
+        def transpose_xn(n):
             if not live(n):
                 return
-            row = work3.tile([P, P], F32)
-            nc.scalar.copy(out=row[:], in_=rstd_psum[n][:])
-            rstd_row[n] = row
+            words = xn[n][:].rearrange("r u p e -> r (u p e)").bitcast(F32)
+            x_t = psum.tile([P, 2, P], F32, name="xn_t")
+            for u in range(2):
+                nc.tensor.transpose(x_t[:, u, :], words[:, P * u : P * (u + 1)], ident_f32[:])
+            xn_t[n] = x_t
 
-        def normalise(n):
+        def copy_xn(n):
             if not live(n):
                 return
             xn_g = work2.tile([P, P, PACK], BF16, align_bytes=64, name="xn_grouped")
-            nc.vector.tensor_tensor(
-                out=xn_g[:],
-                in0=x_mid_t[n][:].rearrange("p t r -> p r t"),
-                in1=rstd_row[n][:].unsqueeze(2).to_broadcast([P, P, PACK]),
-                op=ALU.mult,
+            nc.scalar.copy(
+                out=xn_g[:].rearrange("p r t -> p (r t)").bitcast(F32).rearrange("p (r u) -> p r u", u=2),
+                in_=xn_t[n][:].rearrange("p u r -> p r u"),
             )
             xn_grouped[n] = xn_g
 
@@ -256,7 +253,7 @@ def tile_shepherdembryo_pb_t_kernel(
             if not live(n):
                 return
             xn_codes, xn_scales = xn_mx[n]
-            h_ps = psum.tile([P, F], F32, bufs=1)
+            h_ps = psum.tile([P, F], F32)
             nc.tensor.matmul_mx(
                 out=h_ps[:],
                 lhsT=xn_codes[:].bitcast(FP8X4),
@@ -290,16 +287,15 @@ def tile_shepherdembryo_pb_t_kernel(
             load_y(n + LOAD_AHEAD)
             if n % CHUNK == 0:
                 load_x(n // CHUNK + 1)
+            scale_xn(n - LAG_SCALE)
             project(n - LAG_PROJECT)
             up_project(n - LAG_UP)
-            spread_inverse_rms(n - LAG_XN)
             transpose_y(n)
-            transpose_x_mid(n - LAG_NORM)
-            sum_squares(n - LAG_NORM)
-            copy_inverse_rms(n - LAG_XN)
-            normalise(n - LAG_XN)
+            transpose_xn(n - LAG_XN)
+            quantise_xn(n - LAG_QUANTISE_XN)
             quantise_y(n)
-            quantise_xn(n - LAG_XN)
             relu(n - LAG_UP)
+            sum_squares(n - LAG_NORM)
             inverse_rms(n - LAG_NORM)
             square_and_store(n - LAG_UP)
+            copy_xn(n - LAG_XN)

@@ -27,6 +27,7 @@ CHUNK = 4
 PAIR = 2
 CHUNKS = TILES // CHUNK
 
+LAG_QUANTISE_Y = 1
 LAG_PROJECT = 2
 LAG_NORM = 3
 LAG_SCALE = 4
@@ -112,6 +113,7 @@ def tile_shepherdembryo_pb_t_kernel(
 
         y_grouped = {}
         y_mx = {}
+        gained = {}
         x_mid = {}
         sumsq = {}
         rstd = {}
@@ -162,7 +164,6 @@ def tile_shepherdembryo_pb_t_kernel(
         def project(n):
             if not live(n):
                 return
-            c, i = divmod(n, CHUNK)
             y_codes, y_scales = y_mx[n]
             attn = psum.tile([P, D], F32)
             for g in range(KG):
@@ -175,13 +176,19 @@ def tile_shepherdembryo_pb_t_kernel(
                     start=(g == 0),
                     stop=(g == KG - 1),
                 )
-            scaled = work3.tile([P, D], F32)
-            nc.vector.tensor_tensor(out=scaled[:], in0=attn[:], in1=gain[:], op=ALU.mult)
+            gained_n = work3.tile([P, D], F32, name="gained")
+            nc.vector.tensor_tensor(out=gained_n[:], in0=attn[:], in1=gain[:], op=ALU.mult)
+            gained[n] = gained_n
+
+        def add_residual(n):
+            if not live(n):
+                return
+            c, i = divmod(n, CHUNK)
             pair, a = divmod(n, PAIR)
             if a == 0:
                 x_mid_pair = outs.tile([P, PAIR, D], F32)
                 x_mid[pair] = x_mid_pair
-            nc.gpsimd.tensor_tensor(out=x_mid[pair][:, a, :], in0=scaled[:], in1=x_sb[c][:, i, :], op=ALU.add)
+            nc.vector.tensor_tensor(out=x_mid[pair][:, a, :], in0=gained[n][:], in1=x_sb[c][:, i, :], op=ALU.add)
             if a == PAIR - 1:
                 b, first = divmod(pair * PAIR, SLOTS)
                 nc.sync.dma_start(out=x_mid_view[b, :, first : first + PAIR, :], in_=x_mid[pair][:])
@@ -287,13 +294,14 @@ def tile_shepherdembryo_pb_t_kernel(
             load_y(n + LOAD_AHEAD)
             if n % CHUNK == 0:
                 load_x(n // CHUNK + 1)
-            scale_xn(n - LAG_SCALE)
             project(n - LAG_PROJECT)
             up_project(n - LAG_UP)
+            quantise_y(n - LAG_QUANTISE_Y)
+            add_residual(n - LAG_PROJECT)
+            scale_xn(n - LAG_SCALE)
+            quantise_xn(n - LAG_QUANTISE_XN)
             transpose_y(n)
             transpose_xn(n - LAG_XN)
-            quantise_xn(n - LAG_QUANTISE_XN)
-            quantise_y(n)
             relu(n - LAG_UP)
             sum_squares(n - LAG_NORM)
             inverse_rms(n - LAG_NORM)

@@ -27,14 +27,14 @@ CHUNK = 4
 PAIR = 2
 CHUNKS = TILES // CHUNK
 
-LAG_QUANTISE_Y = 1
-LAG_PROJECT = 2
+PAIRS = TILES // PAIR
+LOAD_AHEAD = 3
+
+LAG_PROJECT = 1
+LAG_ADD = 2
 LAG_NORM = 3
-LAG_SCALE = 4
-LAG_XN = 5
-LAG_QUANTISE_XN = 6
-LAG_UP = 7
-LOAD_AHEAD = 6
+LAG_XN = 4
+LAG_UP = 5
 
 
 def tile_shepherdembryo_pb_t_kernel(
@@ -51,8 +51,7 @@ def tile_shepherdembryo_pb_t_kernel(
         resident = ctx.enter_context(tc.tile_pool(name="resident", bufs=1))
         work2 = ctx.enter_context(tc.tile_pool(name="work2", bufs=2))
         work3 = ctx.enter_context(tc.tile_pool(name="work3", bufs=3))
-        work4 = ctx.enter_context(tc.tile_pool(name="work4", bufs=4))
-        outs = ctx.enter_context(tc.tile_pool(name="outs", bufs=7))
+        outs = ctx.enter_context(tc.tile_pool(name="outs", bufs=6))
         psum = ctx.enter_context(tc.psum_pool(name="psum", bufs=2))
         ctx.enter_context(tc.manual_schedule())
 
@@ -99,7 +98,7 @@ def tile_shepherdembryo_pb_t_kernel(
             )
         nc.sync.dma_start(out=gain[:], in_=attn_scale.partition_broadcast(P))
         load_x(0)
-        for n in range(2, LOAD_AHEAD):
+        for n in range(2, PAIR * LOAD_AHEAD):
             load_y(n)
         nc.sync.dma_start(
             out=wfc_words[:].bitcast(I32),
@@ -111,8 +110,10 @@ def tile_shepherdembryo_pb_t_kernel(
                 in_=w_fc_scales[0, 4 * quad : 4 * quad + 4, :].bitcast(I32),
             )
 
+        y_psum = {}
         y_grouped = {}
         y_mx = {}
+        attn_psum = {}
         gained = {}
         x_mid = {}
         sumsq = {}
@@ -124,186 +125,198 @@ def tile_shepherdembryo_pb_t_kernel(
         h_psum = {}
         h_sb = {}
 
-        def live(n):
-            return 0 <= n < TILES
+        def live(m):
+            return 0 <= m < PAIRS
 
-        def transpose_y(n):
-            if not live(n):
+        def transpose_y(m):
+            if not live(m):
                 return
-            words = y_sb[n][:].rearrange("p h j -> p (h j)").bitcast(F32)
-            y_t = psum.tile([P, KG, 2, P], F32)
-            for g in range(KG):
-                for u in range(2):
-                    nc.tensor.transpose(
-                        y_t[:, g, u, :],
-                        words[:, (K_PASS // 2) * g + u : (K_PASS // 2) * (g + 1) : 2],
-                        ident_f32[:],
-                    )
-            y_g = work2.tile([P, KG, P, PACK], BF16, align_bytes=64, name="y_grouped")
-            nc.vector.tensor_copy(
-                out=y_g[:]
-                .rearrange("p g r t -> p (g r t)")
-                .bitcast(F32)
-                .rearrange("p (g r u) -> p g r u", g=KG, u=2),
-                in_=y_t[:].rearrange("p g u r -> p g r u"),
-            )
-            y_grouped[n] = y_g
+            for n in (PAIR * m, PAIR * m + 1):
+                words = y_sb[n][:].rearrange("p h j -> p (h j)").bitcast(F32)
+                y_t = psum.tile([P, KG, 2, P], F32)
+                for g in range(KG):
+                    for u in range(2):
+                        nc.tensor.transpose(
+                            y_t[:, g, u, :],
+                            words[:, (K_PASS // 2) * g + u : (K_PASS // 2) * (g + 1) : 2],
+                            ident_f32[:],
+                        )
+                y_psum[n] = y_t
 
-        def quantise_y(n):
-            if not live(n):
+        def copy_y(m):
+            if not live(m):
                 return
-            y_codes = work4.tile([P, KG, P], U32, align_bytes=64)
-            y_scales = work4.tile([P, KG, P], U8, align_bytes=64)
-            nc.vector.quantize_mx(
-                out=y_codes[:].rearrange("p g r -> p (g r)").bitcast(FP8X4),
-                scales=y_scales[:].rearrange("p g r -> p (g r)"),
-                in_=y_grouped[n][:].rearrange("p g r t -> p (g r t)"),
-            )
-            y_mx[n] = (y_codes, y_scales)
-
-        def project(n):
-            if not live(n):
-                return
-            y_codes, y_scales = y_mx[n]
-            attn = psum.tile([P, D], F32)
-            for g in range(KG):
-                nc.tensor.matmul_mx(
-                    out=attn[:],
-                    lhsT=y_codes[:, g, :].bitcast(FP8X4),
-                    lhsT_scale=y_scales[:, g, :],
-                    rhs=wo_words[:, g, :].bitcast(FP8X4),
-                    rhs_scale=w_planes[:, g, :],
-                    start=(g == 0),
-                    stop=(g == KG - 1),
+            y_g = work2.tile([P, PAIR, KG, P, PACK], BF16, align_bytes=64, name="y_grouped")
+            words = y_g[:].rearrange("p a g r t -> p (a g r t)").bitcast(F32)
+            words = words.rearrange("p (a g r u) -> p a g r u", a=PAIR, g=KG, u=2)
+            for a in range(PAIR):
+                nc.vector.tensor_copy(
+                    out=words[:, a], in_=y_psum[PAIR * m + a][:].rearrange("p g u r -> p g r u")
                 )
-            gained_n = work3.tile([P, D], F32, name="gained")
-            nc.vector.tensor_tensor(out=gained_n[:], in0=attn[:], in1=gain[:], op=ALU.mult)
-            gained[n] = gained_n
+            y_grouped[m] = y_g
 
-        def add_residual(n):
-            if not live(n):
+        def quantise_y(m):
+            if not live(m):
                 return
-            c, i = divmod(n, CHUNK)
-            pair, a = divmod(n, PAIR)
-            if a == 0:
-                x_mid_pair = outs.tile([P, PAIR, D], F32)
-                x_mid[pair] = x_mid_pair
-            nc.vector.tensor_tensor(out=x_mid[pair][:, a, :], in0=gained[n][:], in1=x_sb[c][:, i, :], op=ALU.add)
-            if a == PAIR - 1:
-                b, first = divmod(pair * PAIR, SLOTS)
-                nc.sync.dma_start(out=x_mid_view[b, :, first : first + PAIR, :], in_=x_mid[pair][:])
-
-        def sum_squares(n):
-            if not live(n):
-                return
-            pair, a = divmod(n, PAIR)
-            squares = work2.tile([P, D], BF16)
-            total = work4.tile([P, 1], F32)
-            nc.scalar.activation(out=squares[:], in_=x_mid[pair][:, a, :], func=ACT.Square, accum_out=total[:])
-            sumsq[n] = total
-
-        def inverse_rms(n):
-            if not live(n):
-                return
-            inv = work4.tile([P, 1], F32)
-            nc.scalar.activation(
-                out=inv[:], in_=sumsq[n][:], func=ACT.Abs_reciprocal_sqrt, bias=eps[:], scale=1.0 / D
-            )
-            rstd[n] = inv
-
-        def scale_xn(n):
-            if not live(n):
-                return
-            pair, a = divmod(n, PAIR)
-            xn_n = work3.tile([P, 2, P, 2], BF16, align_bytes=64, name="xn")
-            nc.vector.tensor_scalar(
-                out=xn_n[:],
-                in0=x_mid[pair][:, a, :].rearrange("r (p u e) -> r u p e", u=2, e=2),
-                scalar1=rstd[n][:],
-                scalar2=None,
-                op0=ALU.mult,
-            )
-            xn[n] = xn_n
-
-        def transpose_xn(n):
-            if not live(n):
-                return
-            words = xn[n][:].rearrange("r u p e -> r (u p e)").bitcast(F32)
-            x_t = psum.tile([P, 2, P], F32, name="xn_t")
-            for u in range(2):
-                nc.tensor.transpose(x_t[:, u, :], words[:, P * u : P * (u + 1)], ident_f32[:])
-            xn_t[n] = x_t
-
-        def copy_xn(n):
-            if not live(n):
-                return
-            xn_g = work2.tile([P, P, PACK], BF16, align_bytes=64, name="xn_grouped")
-            nc.scalar.copy(
-                out=xn_g[:].rearrange("p r t -> p (r t)").bitcast(F32).rearrange("p (r u) -> p r u", u=2),
-                in_=xn_t[n][:].rearrange("p u r -> p r u"),
-            )
-            xn_grouped[n] = xn_g
-
-        def quantise_xn(n):
-            if not live(n):
-                return
-            xn_codes = work4.tile([P, P], U32, align_bytes=64)
-            xn_scales = work4.tile([P, P], U8, align_bytes=64)
+            y_codes = work3.tile([P, PAIR, KG, P], U32, align_bytes=64)
+            y_scales = work3.tile([P, PAIR, KG, P], U8, align_bytes=64)
             nc.vector.quantize_mx(
-                out=xn_codes[:].bitcast(FP8X4),
-                scales=xn_scales[:],
-                in_=xn_grouped[n][:].rearrange("p r t -> p (r t)"),
+                out=y_codes[:].rearrange("p a g r -> p (a g r)").bitcast(FP8X4),
+                scales=y_scales[:].rearrange("p a g r -> p (a g r)"),
+                in_=y_grouped[m][:].rearrange("p a g r t -> p (a g r t)"),
             )
-            xn_mx[n] = (xn_codes, xn_scales)
+            y_mx[m] = (y_codes, y_scales)
 
-        def up_project(n):
-            if not live(n):
+        def project(m):
+            if not live(m):
                 return
-            xn_codes, xn_scales = xn_mx[n]
-            h_ps = psum.tile([P, F], F32)
-            nc.tensor.matmul_mx(
-                out=h_ps[:],
-                lhsT=xn_codes[:].bitcast(FP8X4),
-                lhsT_scale=xn_scales[:],
-                rhs=wfc_words[:].bitcast(FP8X4),
-                rhs_scale=w_planes[:, KG, :],
-                start=True,
-                stop=True,
+            y_codes, y_scales = y_mx[m]
+            for a in range(PAIR):
+                attn = psum.tile([P, D], F32)
+                for g in range(KG):
+                    nc.tensor.matmul_mx(
+                        out=attn[:],
+                        lhsT=y_codes[:, a, g, :].bitcast(FP8X4),
+                        lhsT_scale=y_scales[:, a, g, :],
+                        rhs=wo_words[:, g, :].bitcast(FP8X4),
+                        rhs_scale=w_planes[:, g, :],
+                        start=(g == 0),
+                        stop=(g == KG - 1),
+                    )
+                attn_psum[PAIR * m + a] = attn
+
+        def apply_gain(m):
+            if not live(m):
+                return
+            gained_m = work2.tile([P, PAIR, D], F32, name="gained")
+            for a in range(PAIR):
+                nc.vector.tensor_tensor(
+                    out=gained_m[:, a, :], in0=attn_psum[PAIR * m + a][:], in1=gain[:], op=ALU.mult
+                )
+            gained[m] = gained_m
+
+        def hold_gpsimd(m):
+            if not live(m):
+                return
+            held = work2.tile([P, 2], BF16)
+            nc.gpsimd.tensor_copy(out=held[:], in_=xn[m][:, PAIR - 1, 0, 0, :])
+
+        def add_residual(m):
+            if not live(m):
+                return
+            c, i = divmod(m * PAIR, CHUNK)
+            x_mid_m = outs.tile([P, PAIR, D], F32, name="x_mid")
+            nc.gpsimd.tensor_tensor(
+                out=x_mid_m[:], in0=gained[m][:], in1=x_sb[c][:, i : i + PAIR, :], op=ALU.add
             )
-            h_psum[n] = h_ps
+            x_mid[m] = x_mid_m
+            b, first = divmod(m * PAIR, SLOTS)
+            nc.sync.dma_start(out=x_mid_view[b, :, first : first + PAIR, :], in_=x_mid_m[:])
 
-        def relu(n):
-            if not live(n):
+        def inverse_rms(m):
+            if not live(m):
                 return
-            pair, a = divmod(n, PAIR)
-            if a == 0:
-                h_pair = outs.tile([P, PAIR, F], F32)
-                h_sb[pair] = h_pair
-            nc.scalar.activation(out=h_sb[pair][:, a, :], in_=h_psum[n][:], func=ACT.Relu)
+            squares = work2.tile([P, D], BF16)
+            total = work2.tile([P, PAIR], F32)
+            for a in range(PAIR):
+                nc.scalar.activation(
+                    out=squares[:], in_=x_mid[m][:, a, :], func=ACT.Square, accum_out=total[:, a : a + 1]
+                )
+            inv = work2.tile([P, PAIR], F32)
+            nc.scalar.activation(out=inv[:], in_=total[:], func=ACT.Abs_reciprocal_sqrt, bias=eps[:], scale=1.0 / D)
+            rstd[m] = inv
 
-        def square_and_store(n):
-            if not live(n):
+        def scale_xn(m):
+            if not live(m):
                 return
-            pair, a = divmod(n, PAIR)
-            nc.scalar.activation(out=h_sb[pair][:, a, :], in_=h_sb[pair][:, a, :], func=ACT.Square)
-            if a == PAIR - 1:
-                b, first = divmod(pair * PAIR, SLOTS)
-                nc.sync.dma_start(out=h_view[b, :, first : first + PAIR, :], in_=h_sb[pair][:])
+            xn_m = work2.tile([P, PAIR, 2, P, 2], BF16, align_bytes=64, name="xn")
+            for a in range(PAIR):
+                nc.vector.tensor_scalar(
+                    out=xn_m[:, a],
+                    in0=x_mid[m][:, a, :].rearrange("r (p u e) -> r u p e", u=2, e=2),
+                    scalar1=rstd[m][:, a : a + 1],
+                    scalar2=None,
+                    op0=ALU.mult,
+                )
+            xn[m] = xn_m
 
-        for n in range(TILES + LAG_UP):
-            load_y(n + LOAD_AHEAD)
-            if n % CHUNK == 0:
-                load_x(n // CHUNK + 1)
-            project(n - LAG_PROJECT)
-            up_project(n - LAG_UP)
-            quantise_y(n - LAG_QUANTISE_Y)
-            add_residual(n - LAG_PROJECT)
-            scale_xn(n - LAG_SCALE)
-            quantise_xn(n - LAG_QUANTISE_XN)
-            transpose_y(n)
-            transpose_xn(n - LAG_XN)
-            relu(n - LAG_UP)
-            sum_squares(n - LAG_NORM)
-            inverse_rms(n - LAG_NORM)
-            square_and_store(n - LAG_UP)
-            copy_xn(n - LAG_XN)
+        def transpose_xn(m):
+            if not live(m):
+                return
+            words = xn[m][:].rearrange("r a u p e -> r (a u p e)").bitcast(F32)
+            x_t = psum.tile([P, PAIR, 2, P], F32, name="xn_t")
+            for a in range(PAIR):
+                for u in range(2):
+                    start = (2 * a + u) * P
+                    nc.tensor.transpose(x_t[:, a, u, :], words[:, start : start + P], ident_f32[:])
+            xn_t[m] = x_t
+
+        def copy_xn(m):
+            if not live(m):
+                return
+            xn_g = work2.tile([P, PAIR, P, PACK], BF16, align_bytes=64, name="xn_grouped")
+            words = xn_g[:].rearrange("p a r t -> p (a r t)").bitcast(F32)
+            nc.scalar.copy(
+                out=words.rearrange("p (a r u) -> p a r u", a=PAIR, u=2),
+                in_=xn_t[m][:].rearrange("p a u r -> p a r u"),
+            )
+            xn_grouped[m] = xn_g
+
+        def quantise_xn(m):
+            if not live(m):
+                return
+            xn_codes = work3.tile([P, PAIR, P], U32, align_bytes=64)
+            xn_scales = work3.tile([P, PAIR, P], U8, align_bytes=64)
+            nc.vector.quantize_mx(
+                out=xn_codes[:].rearrange("p a r -> p (a r)").bitcast(FP8X4),
+                scales=xn_scales[:].rearrange("p a r -> p (a r)"),
+                in_=xn_grouped[m][:].rearrange("p a r t -> p (a r t)"),
+            )
+            xn_mx[m] = (xn_codes, xn_scales)
+
+        def up_project(m):
+            if not live(m):
+                return
+            xn_codes, xn_scales = xn_mx[m]
+            for a in range(PAIR):
+                h_ps = psum.tile([P, F], F32)
+                nc.tensor.matmul_mx(
+                    out=h_ps[:],
+                    lhsT=xn_codes[:, a, :].bitcast(FP8X4),
+                    lhsT_scale=xn_scales[:, a, :],
+                    rhs=wfc_words[:].bitcast(FP8X4),
+                    rhs_scale=w_planes[:, KG, :],
+                    start=True,
+                    stop=True,
+                )
+                h_psum[PAIR * m + a] = h_ps
+
+        def squared_relu(m):
+            if not live(m):
+                return
+            h_m = outs.tile([P, PAIR, F], F32, name="h")
+            for a in range(PAIR):
+                nc.scalar.activation(out=h_m[:, a, :], in_=h_psum[PAIR * m + a][:], func=ACT.Relu)
+            nc.scalar.activation(out=h_m[:], in_=h_m[:], func=ACT.Square)
+            b, first = divmod(m * PAIR, SLOTS)
+            nc.sync.dma_start(out=h_view[b, :, first : first + PAIR, :], in_=h_m[:])
+
+        for m in range(PAIRS + LAG_UP):
+            for n in range(PAIR * (m + LOAD_AHEAD), PAIR * (m + LOAD_AHEAD + 1)):
+                load_y(n)
+            if (m * PAIR) % CHUNK == 0:
+                load_x(m * PAIR // CHUNK + 1)
+            transpose_y(m)
+            transpose_xn(m - LAG_XN)
+            project(m - LAG_PROJECT)
+            up_project(m - LAG_UP)
+            copy_y(m)
+            apply_gain(m - LAG_PROJECT)
+            inverse_rms(m - LAG_NORM)
+            copy_xn(m - LAG_XN)
+            hold_gpsimd(m - LAG_XN)
+            add_residual(m - LAG_ADD)
+            quantise_y(m)
+            quantise_xn(m - LAG_XN)
+            scale_xn(m - LAG_NORM)
+            squared_relu(m - LAG_UP)

@@ -30,11 +30,8 @@ CHUNKS = TILES // CHUNK
 PAIRS = TILES // PAIR
 LOAD_AHEAD = 3
 
-LAG_PROJECT = 1
-LAG_ADD = 2
-LAG_NORM = 3
-LAG_XN = 4
-LAG_UP = 5
+FIRST_PAIRS = 2
+LAST_PAIR = PAIRS - 1
 
 
 def tile_shepherdembryo_pb_t_kernel(
@@ -150,9 +147,8 @@ def tile_shepherdembryo_pb_t_kernel(
             words = y_g[:].rearrange("p a g r t -> p (a g r t)").bitcast(F32)
             words = words.rearrange("p (a g r u) -> p a g r u", a=PAIR, g=KG, u=2)
             for a in range(PAIR):
-                nc.vector.tensor_copy(
-                    out=words[:, a], in_=y_psum[PAIR * m + a][:].rearrange("p g u r -> p g r u")
-                )
+                copy = nc.scalar.copy if m < FIRST_PAIRS and a == 1 else nc.vector.tensor_copy
+                copy(out=words[:, a], in_=y_psum[PAIR * m + a][:].rearrange("p g u r -> p g r u"))
             y_grouped[m] = y_g
 
         def quantise_y(m):
@@ -196,17 +192,13 @@ def tile_shepherdembryo_pb_t_kernel(
             gained[m] = gained_m
 
         def hold_gpsimd(m):
-            if not live(m):
-                return
-            held = work2.tile([P, 2], BF16)
-            nc.gpsimd.tensor_copy(out=held[:], in_=xn[m][:, PAIR - 1, 0, 0, :])
+            held = work2.tile([P, 1], U32)
+            nc.gpsimd.tensor_copy(out=held[:], in_=y_mx[m][0][:, PAIR - 1, KG - 1, P - 1 : P])
 
-        def add_residual(m):
-            if not live(m):
-                return
+        def add_residual(m, engine):
             c, i = divmod(m * PAIR, CHUNK)
             x_mid_m = outs.tile([P, PAIR, D], F32, name="x_mid")
-            nc.gpsimd.tensor_tensor(
+            engine.tensor_tensor(
                 out=x_mid_m[:], in0=gained[m][:], in1=x_sb[c][:, i : i + PAIR, :], op=ALU.add
             )
             x_mid[m] = x_mid_m
@@ -301,22 +293,56 @@ def tile_shepherdembryo_pb_t_kernel(
             b, first = divmod(m * PAIR, SLOTS)
             nc.sync.dma_start(out=h_view[b, :, first : first + PAIR, :], in_=h_m[:])
 
-        for m in range(PAIRS + LAG_UP):
-            for n in range(PAIR * (m + LOAD_AHEAD), PAIR * (m + LOAD_AHEAD + 1)):
+        def squared_relu_shared(m):
+            h_m = outs.tile([P, PAIR, F], F32, name="h")
+            b, first = divmod(m * PAIR, SLOTS)
+            nc.scalar.activation(out=h_m[:, 0, :], in_=h_psum[PAIR * m][:], func=ACT.Relu)
+            nc.vector.tensor_scalar(
+                out=h_m[:, 1, :], in0=h_psum[PAIR * m + 1][:], scalar1=0.0, scalar2=None, op0=ALU.max
+            )
+            nc.scalar.activation(out=h_m[:, 0, :], in_=h_m[:, 0, :], func=ACT.Square)
+            nc.vector.tensor_tensor(out=h_m[:, 1, :], in0=h_m[:, 1, :], in1=h_m[:, 1, :], op=ALU.mult)
+            for a in range(PAIR):
+                nc.sync.dma_start(out=h_view[b, :, first + a, :], in_=h_m[:, a, :])
+
+        def add_turn(m):
+            return m + 1 if m < FIRST_PAIRS or m == LAST_PAIR else m + 2
+
+        def at(turn, lag):
+            return [m for m in range(PAIRS) if add_turn(m) + lag == turn]
+
+        for turn in range(PAIRS + 5):
+            for n in range(PAIR * (turn + LOAD_AHEAD), PAIR * (turn + LOAD_AHEAD + 1)):
                 load_y(n)
-            if (m * PAIR) % CHUNK == 0:
-                load_x(m * PAIR // CHUNK + 1)
-            transpose_y(m)
-            transpose_xn(m - LAG_XN)
-            project(m - LAG_PROJECT)
-            up_project(m - LAG_UP)
-            copy_y(m)
-            apply_gain(m - LAG_PROJECT)
-            inverse_rms(m - LAG_NORM)
-            copy_xn(m - LAG_XN)
-            hold_gpsimd(m - LAG_XN)
-            add_residual(m - LAG_ADD)
-            quantise_y(m)
-            quantise_xn(m - LAG_XN)
-            scale_xn(m - LAG_NORM)
-            squared_relu(m - LAG_UP)
+            if (turn * PAIR) % CHUNK == 0:
+                load_x(turn * PAIR // CHUNK + 1)
+            transpose_y(turn)
+            for m in at(turn, 2):
+                transpose_xn(m)
+            for m in at(turn, 3):
+                up_project(m)
+            project(turn - 1)
+            copy_y(turn)
+            for m in at(turn, 2):
+                copy_xn(m)
+            for m in at(turn, 3):
+                if turn < PAIRS:
+                    squared_relu(m)
+            apply_gain(turn - 1)
+            for m in at(turn, 0):
+                if m < FIRST_PAIRS or m == LAST_PAIR:
+                    add_residual(m, nc.vector)
+                else:
+                    if live(turn - 1):
+                        hold_gpsimd(turn - 1)
+                    add_residual(m, nc.gpsimd)
+            for m in at(turn, 1):
+                scale_xn(m)
+            for m in at(turn, 2):
+                quantise_xn(m)
+            quantise_y(turn)
+            for m in at(turn, 3):
+                if turn >= PAIRS:
+                    squared_relu_shared(m)
+            for m in at(turn, 0):
+                inverse_rms(m)

@@ -32,6 +32,7 @@ LOAD_AHEAD = 3
 
 FIRST_PAIRS = 2
 LAST_PAIR = PAIRS - 1
+GPSIMD_ADDS = 768
 
 
 def tile_shepherdembryo_pb_t_kernel(
@@ -94,8 +95,10 @@ def tile_shepherdembryo_pb_t_kernel(
                 in_=w_o_scales[:, 4 * quad : 4 * quad + 4, :].rearrange("g r n -> r g n").bitcast(I32),
             )
         nc.sync.dma_start(out=gain[:], in_=attn_scale.partition_broadcast(P))
+        load_y(2)
+        load_y(3)
         load_x(0)
-        for n in range(2, PAIR * LOAD_AHEAD):
+        for n in range(4, PAIR * LOAD_AHEAD):
             load_y(n)
         nc.sync.dma_start(
             out=wfc_words[:].bitcast(I32),
@@ -147,7 +150,7 @@ def tile_shepherdembryo_pb_t_kernel(
             words = y_g[:].rearrange("p a g r t -> p (a g r t)").bitcast(F32)
             words = words.rearrange("p (a g r u) -> p a g r u", a=PAIR, g=KG, u=2)
             for a in range(PAIR):
-                copy = nc.scalar.copy if m < FIRST_PAIRS and a == 1 else nc.vector.tensor_copy
+                copy = nc.scalar.copy if m < FIRST_PAIRS and (m, a) != (0, 0) else nc.vector.tensor_copy
                 copy(out=words[:, a], in_=y_psum[PAIR * m + a][:].rearrange("p g u r -> p g r u"))
             y_grouped[m] = y_g
 
@@ -195,27 +198,37 @@ def tile_shepherdembryo_pb_t_kernel(
             held = work2.tile([P, 1], U32)
             nc.gpsimd.tensor_copy(out=held[:], in_=y_mx[m][0][:, PAIR - 1, KG - 1, P - 1 : P])
 
-        def add_residual(m, engine):
+        def add_part(m, engine, lo, hi):
             c, i = divmod(m * PAIR, CHUNK)
-            x_mid_m = outs.tile([P, PAIR, D], F32, name="x_mid")
             engine.tensor_tensor(
-                out=x_mid_m[:], in0=gained[m][:], in1=x_sb[c][:, i : i + PAIR, :], op=ALU.add
+                out=x_mid[m][:].rearrange("p a d -> p (a d)")[:, lo:hi],
+                in0=gained[m][:].rearrange("p a d -> p (a d)")[:, lo:hi],
+                in1=x_sb[c][:, i : i + PAIR, :].rearrange("p a d -> p (a d)")[:, lo:hi],
+                op=ALU.add,
             )
+
+        def add_alloc(m):
+            x_mid_m = outs.tile([P, PAIR, D], F32, name="x_mid")
             x_mid[m] = x_mid_m
+
+        def store_x_mid(m):
             b, first = divmod(m * PAIR, SLOTS)
-            nc.sync.dma_start(out=x_mid_view[b, :, first : first + PAIR, :], in_=x_mid_m[:])
+            nc.sync.dma_start(out=x_mid_view[b, :, first : first + PAIR, :], in_=x_mid[m][:])
+
+        def sum_squares(m, a):
+            if a == 0:
+                total = work2.tile([P, PAIR], F32)
+                sumsq[m] = total
+            squares = work2.tile([P, D], BF16)
+            nc.scalar.activation(
+                out=squares[:], in_=x_mid[m][:, a, :], func=ACT.Square, accum_out=sumsq[m][:, a : a + 1]
+            )
 
         def inverse_rms(m):
-            if not live(m):
-                return
-            squares = work2.tile([P, D], BF16)
-            total = work2.tile([P, PAIR], F32)
-            for a in range(PAIR):
-                nc.scalar.activation(
-                    out=squares[:], in_=x_mid[m][:, a, :], func=ACT.Square, accum_out=total[:, a : a + 1]
-                )
             inv = work2.tile([P, PAIR], F32)
-            nc.scalar.activation(out=inv[:], in_=total[:], func=ACT.Abs_reciprocal_sqrt, bias=eps[:], scale=1.0 / D)
+            nc.scalar.activation(
+                out=inv[:], in_=sumsq[m][:], func=ACT.Abs_reciprocal_sqrt, bias=eps[:], scale=1.0 / D
+            )
             rstd[m] = inv
 
         def scale_xn(m):
@@ -283,15 +296,16 @@ def tile_shepherdembryo_pb_t_kernel(
                 )
                 h_psum[PAIR * m + a] = h_ps
 
-        def squared_relu(m):
-            if not live(m):
-                return
-            h_m = outs.tile([P, PAIR, F], F32, name="h")
-            for a in range(PAIR):
-                nc.scalar.activation(out=h_m[:, a, :], in_=h_psum[PAIR * m + a][:], func=ACT.Relu)
-            nc.scalar.activation(out=h_m[:], in_=h_m[:], func=ACT.Square)
+        def relu(m, a):
+            if a == 0:
+                h_m = outs.tile([P, PAIR, F], F32, name="h")
+                h_sb[m] = h_m
+            nc.scalar.activation(out=h_sb[m][:, a, :], in_=h_psum[PAIR * m + a][:], func=ACT.Relu)
+
+        def square(m):
+            nc.scalar.activation(out=h_sb[m][:], in_=h_sb[m][:], func=ACT.Square)
             b, first = divmod(m * PAIR, SLOTS)
-            nc.sync.dma_start(out=h_view[b, :, first : first + PAIR, :], in_=h_m[:])
+            nc.sync.dma_start(out=h_view[b, :, first : first + PAIR, :], in_=h_sb[m][:])
 
         def squared_relu_shared(m):
             h_m = outs.tile([P, PAIR, F], F32, name="h")
@@ -311,31 +325,56 @@ def tile_shepherdembryo_pb_t_kernel(
         def at(turn, lag):
             return [m for m in range(PAIRS) if add_turn(m) + lag == turn]
 
+        def scalar_turn(turn):
+            norm, xns, ups, sqs = at(turn, 1), at(turn, 2), at(turn, 3), at(turn, 4)
+            for m in norm:
+                sum_squares(m, 0)
+                sum_squares(m, 1)
+            if turn <= PAIRS:
+                for m in sqs:
+                    square(m)
+            for m in xns:
+                copy_xn(m)
+            for m in norm:
+                inverse_rms(m)
+            if turn < PAIRS:
+                for m in ups:
+                    relu(m, 0)
+                    relu(m, 1)
+
         for turn in range(PAIRS + 5):
             for n in range(PAIR * (turn + LOAD_AHEAD), PAIR * (turn + LOAD_AHEAD + 1)):
                 load_y(n)
             if (turn * PAIR) % CHUNK == 0:
                 load_x(turn * PAIR // CHUNK + 1)
+            if turn <= 1:
+                project(turn - 1)
             transpose_y(turn)
             for m in at(turn, 2):
                 transpose_xn(m)
             for m in at(turn, 3):
                 up_project(m)
-            project(turn - 1)
+            if turn > 1:
+                project(turn - 1)
+            if turn <= 1:
+                apply_gain(turn - 1)
             copy_y(turn)
-            for m in at(turn, 2):
-                copy_xn(m)
-            for m in at(turn, 3):
-                if turn < PAIRS:
-                    squared_relu(m)
-            apply_gain(turn - 1)
+            if turn >= PAIRS:
+                scalar_turn(turn)
+            if turn > 1:
+                apply_gain(turn - 1)
             for m in at(turn, 0):
+                add_alloc(m)
                 if m < FIRST_PAIRS or m == LAST_PAIR:
-                    add_residual(m, nc.vector)
+                    add_part(m, nc.vector, 0, PAIR * D)
                 else:
                     if live(turn - 1):
                         hold_gpsimd(turn - 1)
-                    add_residual(m, nc.gpsimd)
+                    add_part(m, nc.gpsimd, PAIR * D - GPSIMD_ADDS, PAIR * D)
+                    add_part(m, nc.vector, 0, PAIR * D - GPSIMD_ADDS)
+                store_x_mid(m)
+            if turn < PAIRS:
+                scalar_turn(turn)
             for m in at(turn, 1):
                 scale_xn(m)
             for m in at(turn, 2):
@@ -344,5 +383,3 @@ def tile_shepherdembryo_pb_t_kernel(
             for m in at(turn, 3):
                 if turn >= PAIRS:
                     squared_relu_shared(m)
-            for m in at(turn, 0):
-                inverse_rms(m)

@@ -28,11 +28,12 @@ PAIR = 2
 CHUNKS = TILES // CHUNK
 
 PAIRS = TILES // PAIR
-LOAD_AHEAD = 3
+LOAD_AHEAD = 4
 
 FIRST_PAIRS = 2
 LAST_PAIR = PAIRS - 1
-GPSIMD_ADDS = 768
+GPSIMD_ADDS = 832
+SCALAR_COPIES = 3
 
 
 def tile_shepherdembryo_pb_t_kernel(
@@ -150,7 +151,7 @@ def tile_shepherdembryo_pb_t_kernel(
             words = y_g[:].rearrange("p a g r t -> p (a g r t)").bitcast(F32)
             words = words.rearrange("p (a g r u) -> p a g r u", a=PAIR, g=KG, u=2)
             for a in range(PAIR):
-                copy = nc.scalar.copy if m < FIRST_PAIRS and (m, a) != (0, 0) else nc.vector.tensor_copy
+                copy = nc.scalar.copy if m < SCALAR_COPIES and (m, a) != (0, 0) else nc.vector.tensor_copy
                 copy(out=words[:, a], in_=y_psum[PAIR * m + a][:].rearrange("p g u r -> p g r u"))
             y_grouped[m] = y_g
 
@@ -296,28 +297,31 @@ def tile_shepherdembryo_pb_t_kernel(
                 )
                 h_psum[PAIR * m + a] = h_ps
 
-        def relu(m, a):
-            if a == 0:
+        def relu(m, on_vector):
+            if m not in h_sb:
                 h_m = outs.tile([P, PAIR, F], F32, name="h")
                 h_sb[m] = h_m
-            nc.scalar.activation(out=h_sb[m][:, a, :], in_=h_psum[PAIR * m + a][:], func=ACT.Relu)
-
-        def square(m):
-            nc.scalar.activation(out=h_sb[m][:], in_=h_sb[m][:], func=ACT.Square)
-            b, first = divmod(m * PAIR, SLOTS)
-            nc.sync.dma_start(out=h_view[b, :, first : first + PAIR, :], in_=h_sb[m][:])
-
-        def squared_relu_shared(m):
-            h_m = outs.tile([P, PAIR, F], F32, name="h")
-            b, first = divmod(m * PAIR, SLOTS)
-            nc.scalar.activation(out=h_m[:, 0, :], in_=h_psum[PAIR * m][:], func=ACT.Relu)
-            nc.vector.tensor_scalar(
-                out=h_m[:, 1, :], in0=h_psum[PAIR * m + 1][:], scalar1=0.0, scalar2=None, op0=ALU.max
-            )
-            nc.scalar.activation(out=h_m[:, 0, :], in_=h_m[:, 0, :], func=ACT.Square)
-            nc.vector.tensor_tensor(out=h_m[:, 1, :], in0=h_m[:, 1, :], in1=h_m[:, 1, :], op=ALU.mult)
             for a in range(PAIR):
-                nc.sync.dma_start(out=h_view[b, :, first + a, :], in_=h_m[:, a, :])
+                h_a, h_ps = h_sb[m][:, a, :], h_psum[PAIR * m + a]
+                if a == 1 and is_shared(m):
+                    if on_vector:
+                        nc.vector.tensor_scalar(out=h_a, in0=h_ps[:], scalar1=0.0, scalar2=None, op0=ALU.max)
+                elif not on_vector:
+                    nc.scalar.activation(out=h_a, in_=h_ps[:], func=ACT.Relu)
+
+        def square(m, on_vector):
+            b, first = divmod(m * PAIR, SLOTS)
+            h = h_sb[m]
+            if not is_shared(m):
+                if not on_vector:
+                    nc.scalar.activation(out=h[:], in_=h[:], func=ACT.Square)
+                    nc.sync.dma_start(out=h_view[b, :, first : first + PAIR, :], in_=h[:])
+            elif not on_vector:
+                nc.scalar.activation(out=h[:, 0, :], in_=h[:, 0, :], func=ACT.Square)
+                nc.sync.dma_start(out=h_view[b, :, first, :], in_=h[:, 0, :])
+            else:
+                nc.vector.tensor_tensor(out=h[:, 1, :], in0=h[:, 1, :], in1=h[:, 1, :], op=ALU.mult)
+                nc.sync.dma_start(out=h_view[b, :, first + 1, :], in_=h[:, 1, :])
 
         def add_turn(m):
             return m + 1 if m < FIRST_PAIRS or m == LAST_PAIR else m + 2
@@ -325,39 +329,39 @@ def tile_shepherdembryo_pb_t_kernel(
         def at(turn, lag):
             return [m for m in range(PAIRS) if add_turn(m) + lag == turn]
 
+        def is_shared(m):
+            return add_turn(m) + 3 >= PAIRS
+
         def scalar_turn(turn):
-            norm, xns, ups, sqs = at(turn, 1), at(turn, 2), at(turn, 3), at(turn, 4)
-            for m in norm:
+            for m in at(turn, 1):
                 sum_squares(m, 0)
                 sum_squares(m, 1)
-            if turn <= PAIRS:
-                for m in sqs:
-                    square(m)
-            for m in xns:
-                copy_xn(m)
-            for m in norm:
+            for m in at(turn, 4):
+                square(m, False)
+            for m in at(turn, 1):
                 inverse_rms(m)
-            if turn < PAIRS:
-                for m in ups:
-                    relu(m, 0)
-                    relu(m, 1)
+            for m in at(turn, 2):
+                copy_xn(m)
+            for m in at(turn, 3):
+                relu(m, False)
 
         for turn in range(PAIRS + 5):
             for n in range(PAIR * (turn + LOAD_AHEAD), PAIR * (turn + LOAD_AHEAD + 1)):
                 load_y(n)
             if (turn * PAIR) % CHUNK == 0:
                 load_x(turn * PAIR // CHUNK + 1)
+
             if turn <= 1:
                 project(turn - 1)
+                apply_gain(turn - 1)
             transpose_y(turn)
             for m in at(turn, 2):
                 transpose_xn(m)
-            for m in at(turn, 3):
-                up_project(m)
             if turn > 1:
                 project(turn - 1)
-            if turn <= 1:
-                apply_gain(turn - 1)
+            for m in at(turn, 3):
+                up_project(m)
+
             copy_y(turn)
             if turn >= PAIRS:
                 scalar_turn(turn)
@@ -375,11 +379,13 @@ def tile_shepherdembryo_pb_t_kernel(
                 store_x_mid(m)
             if turn < PAIRS:
                 scalar_turn(turn)
+
+            for m in at(turn, 4):
+                square(m, True)
             for m in at(turn, 1):
                 scale_xn(m)
+            quantise_y(turn)
             for m in at(turn, 2):
                 quantise_xn(m)
-            quantise_y(turn)
             for m in at(turn, 3):
-                if turn >= PAIRS:
-                    squared_relu_shared(m)
+                relu(m, True)

from contextlib import ExitStack

import concourse.mybir as mybir
from concourse.masks import make_identity

BF16 = mybir.dt.bfloat16
F32 = mybir.dt.float32
I32 = mybir.dt.int32
U32 = mybir.dt.uint32
U8 = mybir.dt.uint8
FP8X4 = mybir.dt.float8_e4m3fn_x4
ALU = mybir.AluOpType
ACT = mybir.ActivationFunctionType

B, S, D, H, DH, F = 2, 2048, 512, 8, 128, 512
E = H * DH
EPS = 1e-6
FLOPS = 2 * B * S * E * D + 2 * B * S * D * F

P = 128
PACK = 4
K_PASS = P * PACK
KG = E // K_PASS
SLOTS = S // P
TILES = B * SLOTS
CHUNK = 4
PAIR = 2
CHUNKS = TILES // CHUNK

PAIRS = TILES // PAIR
LOAD_AHEAD = 4

FIRST_PAIRS = 2
LAST_PAIR = PAIRS - 1
GPSIMD_ADDS = 832
SCALAR_COPIES = 3


def tile_shepherdembryo_pb_t_kernel(
    tc, y_attn, x, w_o_words, w_o_scales, attn_scale, w_fc_words, w_fc_scales, out_0, out_1
):
    nc = tc.nc
    y_view = y_attn.rearrange("b h (p i) j -> b p h i j", i=SLOTS)
    x_view = x.rearrange("b (p i) d -> b p i d", i=SLOTS)
    x_mid_view = out_0.rearrange("b (p i) d -> b p i d", i=SLOTS)
    h_view = out_1.rearrange("b (p i) d -> b p i d", i=SLOTS)

    with ExitStack() as ctx:
        const = ctx.enter_context(tc.tile_pool(name="const", bufs=1))
        resident = ctx.enter_context(tc.tile_pool(name="resident", bufs=1))
        work2 = ctx.enter_context(tc.tile_pool(name="work2", bufs=2))
        work3 = ctx.enter_context(tc.tile_pool(name="work3", bufs=3))
        outs = ctx.enter_context(tc.tile_pool(name="outs", bufs=6))
        psum = ctx.enter_context(tc.psum_pool(name="psum", bufs=2))
        ctx.enter_context(tc.manual_schedule())

        ident_f32 = const.tile([P, P], F32)
        make_identity(nc, ident_f32[:])
        eps = const.tile([P, 1], F32)
        nc.vector.memset(eps[:], EPS)
        w_planes = const.tile([P, KG + 1, D], U8, align_bytes=64)
        nc.vector.memset(w_planes[:].rearrange("p w n -> p (w n)").bitcast(I32), 0)
        wo_words = const.tile([P, KG, D], U32, align_bytes=64)
        wfc_words = const.tile([P, F], U32, align_bytes=64)
        gain = const.tile([P, D], BF16)

        y_sb = {}
        x_sb = {}

        def load_y(n):
            if n >= TILES:
                return
            b, i = divmod(n, SLOTS)
            y_n = resident.tile([P, H, DH], BF16, name="y_sb%d" % n)
            nc.sync.dma_start(out=y_n[:], in_=y_view[b, :, :, i, :])
            y_sb[n] = y_n

        def load_x(c):
            if c >= CHUNKS:
                return
            b, first = divmod(c * CHUNK, SLOTS)
            x_c = resident.tile([P, CHUNK, D], BF16, name="x_sb%d" % c)
            nc.sync.dma_start(out=x_c[:], in_=x_view[b, :, first : first + CHUNK, :])
            x_sb[c] = x_c

        load_y(0)
        load_y(1)
        for g in range(KG):
            nc.sync.dma_start(
                out=wo_words[:, g, :].bitcast(I32),
                in_=w_o_words[g].rearrange("p n t -> p (n t)").bitcast(I32),
            )
        for quad in range(4):
            nc.sync.dma_start(
                out=w_planes[32 * quad : 32 * quad + 4, 0:KG, :].bitcast(I32),
                in_=w_o_scales[:, 4 * quad : 4 * quad + 4, :].rearrange("g r n -> r g n").bitcast(I32),
            )
        nc.sync.dma_start(out=gain[:], in_=attn_scale.partition_broadcast(P))
        load_y(2)
        load_y(3)
        load_x(0)
        for n in range(4, PAIR * LOAD_AHEAD):
            load_y(n)
        nc.sync.dma_start(
            out=wfc_words[:].bitcast(I32),
            in_=w_fc_words[0].rearrange("p n t -> p (n t)").bitcast(I32),
        )
        for quad in range(4):
            nc.sync.dma_start(
                out=w_planes[32 * quad : 32 * quad + 4, KG, :].bitcast(I32),
                in_=w_fc_scales[0, 4 * quad : 4 * quad + 4, :].bitcast(I32),
            )

        y_psum = {}
        y_grouped = {}
        y_mx = {}
        attn_psum = {}
        gained = {}
        x_mid = {}
        sumsq = {}
        rstd = {}
        xn = {}
        xn_t = {}
        xn_grouped = {}
        xn_mx = {}
        h_psum = {}
        h_sb = {}

        def live(m):
            return 0 <= m < PAIRS

        def transpose_y(m):
            if not live(m):
                return
            for n in (PAIR * m, PAIR * m + 1):
                words = y_sb[n][:].rearrange("p h j -> p (h j)").bitcast(F32)
                y_t = psum.tile([P, KG, 2, P], F32)
                for g in range(KG):
                    for u in range(2):
                        nc.tensor.transpose(
                            y_t[:, g, u, :],
                            words[:, (K_PASS // 2) * g + u : (K_PASS // 2) * (g + 1) : 2],
                            ident_f32[:],
                        )
                y_psum[n] = y_t

        def copy_y(m):
            if not live(m):
                return
            y_g = work2.tile([P, PAIR, KG, P, PACK], BF16, align_bytes=64, name="y_grouped")
            words = y_g[:].rearrange("p a g r t -> p (a g r t)").bitcast(F32)
            words = words.rearrange("p (a g r u) -> p a g r u", a=PAIR, g=KG, u=2)
            for a in range(PAIR):
                copy = nc.scalar.copy if m < SCALAR_COPIES and (m, a) != (0, 0) else nc.vector.tensor_copy
                copy(out=words[:, a], in_=y_psum[PAIR * m + a][:].rearrange("p g u r -> p g r u"))
            y_grouped[m] = y_g

        def quantise_y(m):
            if not live(m):
                return
            y_codes = work3.tile([P, PAIR, KG, P], U32, align_bytes=64)
            y_scales = work3.tile([P, PAIR, KG, P], U8, align_bytes=64)
            nc.vector.quantize_mx(
                out=y_codes[:].rearrange("p a g r -> p (a g r)").bitcast(FP8X4),
                scales=y_scales[:].rearrange("p a g r -> p (a g r)"),
                in_=y_grouped[m][:].rearrange("p a g r t -> p (a g r t)"),
            )
            y_mx[m] = (y_codes, y_scales)

        def project(m):
            if not live(m):
                return
            y_codes, y_scales = y_mx[m]
            for a in range(PAIR):
                attn = psum.tile([P, D], F32)
                for g in range(KG):
                    nc.tensor.matmul_mx(
                        out=attn[:],
                        lhsT=y_codes[:, a, g, :].bitcast(FP8X4),
                        lhsT_scale=y_scales[:, a, g, :],
                        rhs=wo_words[:, g, :].bitcast(FP8X4),
                        rhs_scale=w_planes[:, g, :],
                        start=(g == 0),
                        stop=(g == KG - 1),
                    )
                attn_psum[PAIR * m + a] = attn

        def apply_gain(m):
            if not live(m):
                return
            gained_m = work2.tile([P, PAIR, D], F32, name="gained")
            for a in range(PAIR):
                nc.vector.tensor_tensor(
                    out=gained_m[:, a, :], in0=attn_psum[PAIR * m + a][:], in1=gain[:], op=ALU.mult
                )
            gained[m] = gained_m

        def hold_gpsimd(m):
            held = work2.tile([P, 1], U32)
            nc.gpsimd.tensor_copy(out=held[:], in_=y_mx[m][0][:, PAIR - 1, KG - 1, P - 1 : P])

        def add_part(m, engine, lo, hi):
            c, i = divmod(m * PAIR, CHUNK)
            engine.tensor_tensor(
                out=x_mid[m][:].rearrange("p a d -> p (a d)")[:, lo:hi],
                in0=gained[m][:].rearrange("p a d -> p (a d)")[:, lo:hi],
                in1=x_sb[c][:, i : i + PAIR, :].rearrange("p a d -> p (a d)")[:, lo:hi],
                op=ALU.add,
            )

        def add_alloc(m):
            x_mid_m = outs.tile([P, PAIR, D], F32, name="x_mid")
            x_mid[m] = x_mid_m

        def store_x_mid(m):
            b, first = divmod(m * PAIR, SLOTS)
            nc.sync.dma_start(out=x_mid_view[b, :, first : first + PAIR, :], in_=x_mid[m][:])

        def sum_squares(m, a):
            if a == 0:
                total = work2.tile([P, PAIR], F32)
                sumsq[m] = total
            squares = work2.tile([P, D], BF16)
            nc.scalar.activation(
                out=squares[:], in_=x_mid[m][:, a, :], func=ACT.Square, accum_out=sumsq[m][:, a : a + 1]
            )

        def inverse_rms(m):
            inv = work2.tile([P, PAIR], F32)
            nc.scalar.activation(
                out=inv[:], in_=sumsq[m][:], func=ACT.Abs_reciprocal_sqrt, bias=eps[:], scale=1.0 / D
            )
            rstd[m] = inv

        def scale_xn(m):
            if not live(m):
                return
            xn_m = work2.tile([P, PAIR, 2, P, 2], BF16, align_bytes=64, name="xn")
            for a in range(PAIR):
                nc.vector.tensor_scalar(
                    out=xn_m[:, a],
                    in0=x_mid[m][:, a, :].rearrange("r (p u e) -> r u p e", u=2, e=2),
                    scalar1=rstd[m][:, a : a + 1],
                    scalar2=None,
                    op0=ALU.mult,
                )
            xn[m] = xn_m

        def transpose_xn(m):
            if not live(m):
                return
            words = xn[m][:].rearrange("r a u p e -> r (a u p e)").bitcast(F32)
            x_t = psum.tile([P, PAIR, 2, P], F32, name="xn_t")
            for a in range(PAIR):
                for u in range(2):
                    start = (2 * a + u) * P
                    nc.tensor.transpose(x_t[:, a, u, :], words[:, start : start + P], ident_f32[:])
            xn_t[m] = x_t

        def copy_xn(m):
            if not live(m):
                return
            xn_g = work2.tile([P, PAIR, P, PACK], BF16, align_bytes=64, name="xn_grouped")
            words = xn_g[:].rearrange("p a r t -> p (a r t)").bitcast(F32)
            nc.scalar.copy(
                out=words.rearrange("p (a r u) -> p a r u", a=PAIR, u=2),
                in_=xn_t[m][:].rearrange("p a u r -> p a r u"),
            )
            xn_grouped[m] = xn_g

        def quantise_xn(m):
            if not live(m):
                return
            xn_codes = work3.tile([P, PAIR, P], U32, align_bytes=64)
            xn_scales = work3.tile([P, PAIR, P], U8, align_bytes=64)
            nc.vector.quantize_mx(
                out=xn_codes[:].rearrange("p a r -> p (a r)").bitcast(FP8X4),
                scales=xn_scales[:].rearrange("p a r -> p (a r)"),
                in_=xn_grouped[m][:].rearrange("p a r t -> p (a r t)"),
            )
            xn_mx[m] = (xn_codes, xn_scales)

        def up_project(m):
            if not live(m):
                return
            xn_codes, xn_scales = xn_mx[m]
            for a in range(PAIR):
                h_ps = psum.tile([P, F], F32)
                nc.tensor.matmul_mx(
                    out=h_ps[:],
                    lhsT=xn_codes[:, a, :].bitcast(FP8X4),
                    lhsT_scale=xn_scales[:, a, :],
                    rhs=wfc_words[:].bitcast(FP8X4),
                    rhs_scale=w_planes[:, KG, :],
                    start=True,
                    stop=True,
                )
                h_psum[PAIR * m + a] = h_ps

        def relu(m, on_vector):
            if m not in h_sb:
                h_m = outs.tile([P, PAIR, F], F32, name="h")
                h_sb[m] = h_m
            for a in range(PAIR):
                h_a, h_ps = h_sb[m][:, a, :], h_psum[PAIR * m + a]
                if a == 1 and is_shared(m):
                    if on_vector:
                        nc.vector.tensor_scalar(out=h_a, in0=h_ps[:], scalar1=0.0, scalar2=None, op0=ALU.max)
                elif not on_vector:
                    nc.scalar.activation(out=h_a, in_=h_ps[:], func=ACT.Relu)

        def square(m, on_vector):
            b, first = divmod(m * PAIR, SLOTS)
            h = h_sb[m]
            if not is_shared(m):
                if not on_vector:
                    nc.scalar.activation(out=h[:], in_=h[:], func=ACT.Square)
                    nc.sync.dma_start(out=h_view[b, :, first : first + PAIR, :], in_=h[:])
            elif not on_vector:
                nc.scalar.activation(out=h[:, 0, :], in_=h[:, 0, :], func=ACT.Square)
                nc.sync.dma_start(out=h_view[b, :, first, :], in_=h[:, 0, :])
            else:
                nc.vector.tensor_tensor(out=h[:, 1, :], in0=h[:, 1, :], in1=h[:, 1, :], op=ALU.mult)
                nc.sync.dma_start(out=h_view[b, :, first + 1, :], in_=h[:, 1, :])

        def add_turn(m):
            return m + 1 if m < FIRST_PAIRS or m == LAST_PAIR else m + 2

        def at(turn, lag):
            return [m for m in range(PAIRS) if add_turn(m) + lag == turn]

        def is_shared(m):
            return add_turn(m) + 3 >= PAIRS

        def scalar_turn(turn):
            for m in at(turn, 1):
                sum_squares(m, 0)
                sum_squares(m, 1)
            for m in at(turn, 4):
                square(m, False)
            for m in at(turn, 1):
                inverse_rms(m)
            for m in at(turn, 2):
                copy_xn(m)
            for m in at(turn, 3):
                relu(m, False)

        for turn in range(PAIRS + 5):
            for n in range(PAIR * (turn + LOAD_AHEAD), PAIR * (turn + LOAD_AHEAD + 1)):
                load_y(n)
            if (turn * PAIR) % CHUNK == 0:
                load_x(turn * PAIR // CHUNK + 1)

            if turn <= 1:
                project(turn - 1)
                apply_gain(turn - 1)
            transpose_y(turn)
            for m in at(turn, 2):
                transpose_xn(m)
            if turn > 1:
                project(turn - 1)
            for m in at(turn, 3):
                up_project(m)

            copy_y(turn)
            if turn >= PAIRS:
                scalar_turn(turn)
            if turn > 1:
                apply_gain(turn - 1)
            for m in at(turn, 0):
                add_alloc(m)
                if m < FIRST_PAIRS or m == LAST_PAIR:
                    add_part(m, nc.vector, 0, PAIR * D)
                else:
                    if live(turn - 1):
                        hold_gpsimd(turn - 1)
                    add_part(m, nc.gpsimd, PAIR * D - GPSIMD_ADDS, PAIR * D)
                    add_part(m, nc.vector, 0, PAIR * D - GPSIMD_ADDS)
                store_x_mid(m)
            if turn < PAIRS:
                scalar_turn(turn)

            for m in at(turn, 4):
                square(m, True)
            for m in at(turn, 1):
                scale_xn(m)
            quantise_y(turn)
            for m in at(turn, 2):
                quantise_xn(m)
            for m in at(turn, 3):
                relu(m, True)
